import numpy as np
import ml_dtypes


def mxq(x, axis, fmt="e4m3"):
    dtype, down = {"e4m3": (ml_dtypes.float8_e4m3fn, 7), "e5m2": (ml_dtypes.float8_e5m2, 14)}[fmt]
    v = np.moveaxis(np.asarray(x, np.float32).astype(ml_dtypes.bfloat16).astype(np.float64), axis, -1)
    blocks = v.reshape(v.shape[:-1] + (-1, 32))
    amax = np.abs(blocks).max(-1, keepdims=True)
    byte = np.maximum(np.where(amax > 0, np.frexp(amax)[1] - 1 + 127, 0) - down, 1)
    scale = np.exp2(byte - 127.0)
    codes = (blocks / scale).astype(np.float32).astype(dtype).astype(np.float64)
    return np.moveaxis((codes * scale).reshape(v.shape), -1, axis)


WIDE = False


def mx_kscale(k):
    if not WIDE:
        return np.ones(k)
    levels = np.array([10, -10, 5, -5, 0])
    if k % 512:
        return np.exp2(np.random.permutation(np.resize(levels, k // 32))).repeat(32)
    a = np.empty((k // 512, 16))
    for p in range(k // 512):
        a[p, :8] = np.random.permutation(np.resize(levels, 8))
        for g in range(8):
            far = levels[np.abs(levels - a[p, g]) >= 10]
            a[p, g + 8] = far[np.random.randint(len(far))]
    return np.exp2(a.ravel()).repeat(32)


BF16 = ml_dtypes.bfloat16


def bf(x):
    return np.asarray(x, np.float32).astype(BF16)


def f64(x):
    return np.asarray(x).astype(np.float64)


B, N, SIZE, CH = 256, 16, 1024, 512


def sigmoid(v):
    return 1.0 / (1.0 + np.exp(-v))


def setup_inputs():
    s = mx_kscale(SIZE)
    half = np.concatenate([np.ones(CH), np.full(CH, 2.0 / np.sqrt(N))])
    return {"z_node": bf(np.random.standard_normal((B, N, SIZE)) * s),
            "z_children": bf(np.random.standard_normal((B, N, SIZE)) * half),
            "W_f": bf(np.random.standard_normal((CH, SIZE)) / np.sqrt(SIZE) / s),
            "U_f": bf(np.random.standard_normal((CH, CH)) / np.sqrt(CH)),
            "b_f": bf(np.random.standard_normal(CH) * 0.5)}


def reference(z_node, z_children, W_f, U_f, b_f):
    h_k = f64(z_children)[..., :CH]
    c_k = f64(z_children)[..., CH:]
    f_j_k = sigmoid((mxq(f64(z_node), 2, "e4m3") @ mxq(f64(W_f), 1, "e4m3").T) + h_k @ f64(U_f).T + f64(b_f))
    return (f_j_k * c_k).sum(axis=1)

@@ -1,0 +1,382 @@
+from contextlib import ExitStack
+
+import concourse.mybir as mybir
+from concourse.masks import make_identity
+
+F32 = mybir.dt.float32
+BF16 = mybir.dt.bfloat16
+U32 = mybir.dt.uint32
+U8 = mybir.dt.uint8
+FP8X4 = mybir.dt.float8_e4m3fn_x4
+ADD = mybir.AluOpType.add
+MULT = mybir.AluOpType.mult
+SIGMOID = mybir.ActivationFunctionType.Sigmoid
+
+P = 128
+B, N, SIZE, CH = 256, 16, 1024, 512
+FLOPS = 2 * B * N * (SIZE + CH) * CH
+
+NPAIR = 16
+PER_HALF = 8
+ACC_MODE = "pe"
+LAG = 3
+BIAS_PE = ()
+TAIL_FREE = True
+NAT_FROM = NPAIR - 1
+
+
+def tile_treelstm_pa_kernel(tc, z_node, z_children, W_f, U_f, b_f, out):
+    nc = tc.nc
+    st = {}
+    with ExitStack() as ctx:
+        const = ctx.enter_context(tc.tile_pool(name="const", bufs=1))
+        data = ctx.enter_context(tc.tile_pool(name="data", bufs=1))
+        work = ctx.enter_context(tc.tile_pool(name="work", bufs=2))
+        psum = ctx.enter_context(tc.psum_pool(name="psum", bufs=1))
+        ctx.enter_context(tc.manual_schedule())
+
+        def bank(tag, bufs):
+            return psum.tile([P, 512], F32, tag=tag, bufs=bufs, name=tag)
+
+        brow = const.tile([P, CH], BF16, name="brow")
+        nc.vector.memset(brow[:], 0.0)
+        nc.scalar.dma_start(out=brow[0:1, :], in_=b_f.rearrange("(o c) -> o c", o=1))
+        ones = const.tile([P, P], BF16, name="ones")
+        nc.vector.memset(ones[:], 1.0)
+        warm = const.tile([P, 8], F32, name="warm")
+        nc.vector.memset(warm[:], 0.0)
+        nc.scalar.activation(out=warm[:], in_=warm[:], func=SIGMOID)
+        ident = const.tile([P, P], F32, name="ident")
+        make_identity(nc, ident[:])
+
+        def load_pair(src, s, nm):
+            bh, j = divmod(s, PER_HALF)
+            t = data.tile([P, 2 * SIZE], BF16, name="%s%d" % (nm, s))
+            nc.sync.dma_start(
+                out=t[:],
+                in_=src[bh * P : (bh + 1) * P, 2 * j : 2 * j + 2, :].rearrange("b n k -> b (n k)"),
+            )
+            return t
+
+        def load_part(s, lo, nm):
+            bh, j = divmod(s, PER_HALF)
+            t = data.tile([P, 2 * CH], BF16, name="%s%d" % (nm, s))
+            nc.sync.dma_start(
+                out=t[:].rearrange("p (t k) -> p t k", t=2),
+                in_=z_children[bh * P : (bh + 1) * P, 2 * j : 2 * j + 2, lo : lo + CH],
+            )
+            return t[:].rearrange("p (t k) -> p t k", t=2)
+
+        def load_children(s):
+            t = load_pair(z_children, s, "zc")[:].rearrange("p (t k) -> p t k", t=2)
+            hid[s] = t[:, :, 0:CH]
+            cel[s] = t[:, :, CH:]
+
+        zn = {}
+        hid = {}
+        cel = {}
+        un = const.tile([P, 4 * CH], BF16, name="un")
+        nc.sync.dma_start(
+            out=un[:].rearrange("p (t k) -> p t k", t=4), in_=U_f.rearrange("(t p) k -> p t k", p=P)
+        )
+        hid[0] = load_part(0, 0, "zh")
+        wn = const.tile([P, 4 * SIZE], BF16, name="wn")
+        nc.sync.dma_start(
+            out=wn[:].rearrange("p (t k) -> p t k", t=4), in_=W_f.rearrange("(t p) k -> p t k", p=P)
+        )
+        zn[0] = load_pair(z_node, 0, "zn")
+        hid[1] = load_part(1, 0, "zh")
+        cel[0] = load_part(0, CH, "zcc")
+        cel[1] = load_part(1, CH, "zcc")
+        for s in range(1, NPAIR):
+            if s + 1 < NPAIR:
+                load_children(s + 1)
+            zn[s] = load_pair(z_node, s, "zn")
+
+        def t_h(s, i):
+            if i == 0:
+                st["hps", s] = bank("hps", 1)
+            tl, v = divmod(i, 2)
+            nc.tensor.transpose(
+                st["hps", s][:, i * P : (i + 1) * P],
+                hid[s][:, tl, :].bitcast(F32)[:, v * P : (v + 1) * P],
+                ident[:],
+            )
+
+        def c_h(s):
+            ht = work.tile([P, 512], F32, tag="ht", bufs=2, name="ht")
+            nc.scalar.copy(out=ht[:], in_=st["hps", s][:])
+            st["ht", s] = ht[:].bitcast(BF16).rearrange("p (t v r e) -> p t v r e", t=2, v=2, e=2)
+
+        def t_z(s, i):
+            tl, wb = divmod(i, 4)
+            if wb == 0:
+                st["zps", s, tl] = bank("zps", 2)
+            nc.tensor.transpose(
+                st["zps", s, tl][:, wb * P : (wb + 1) * P],
+                zn[s][:].bitcast(F32)[:, tl * 512 + (wb // 2) * 256 + wb % 2 : tl * 512 + (wb // 2 + 1) * 256 : 2],
+                ident[:],
+            )
+
+        def c_z(s, tl):
+            if tl == 0:
+                st["zg", s] = work.tile([P, 2048], BF16, tag="zg", bufs=2, name="zg", align_bytes=64)
+            dst = st["zg", s][:].bitcast(F32)[:, tl * 512 : (tl + 1) * 512]
+            nc.scalar.copy(
+                out=dst.rearrange("p (g r u) -> p g r u", g=2, u=2),
+                in_=st["zps", s, tl][:].rearrange("p (g u r) -> p g r u", g=2, u=2),
+            )
+
+        def q_z(s):
+            zq = work.tile([P, 512], U32, tag="zq", bufs=3, name="zq", align_bytes=64)
+            zs = work.tile([P, 512], U8, tag="zs", bufs=3, name="zs", align_bytes=64)
+            nc.vector.quantize_mx(out=zq[:].bitcast(FP8X4), scales=zs[:], in_=st["zg", s][:])
+            st["zq", s] = (zq, zs)
+
+        def bias_on_pe(s, tl):
+            return (2 * s + tl) % 8 in BIAS_PE
+
+        def mm_plain(s, tl, i):
+            if i == 0:
+                st["pl", s, tl] = bank("pl", 2)
+            last = 4 if bias_on_pe(s, tl) else 3
+            if i < 4:
+                v, e = divmod(i, 2)
+                lhs = st["ht", s][:, tl, v, :, e]
+                rhs = ut16[:, v, :, e]
+            else:
+                lhs = ones[:]
+                rhs = brow[:]
+            nc.tensor.matmul(out=st["pl", s, tl][:], lhsT=lhs, rhs=rhs, start=(i == 0), stop=(i == last))
+
+        def mm_mx(s, tl, g):
+            if g == 0:
+                st["mx", s, tl] = bank("mx", 2)
+            zq, zs = st["zq", s]
+            c0 = (tl * 2 + g) * P
+            nc.tensor.matmul_mx(
+                out=st["mx", s, tl][:],
+                lhsT=zq[:, c0 : c0 + P].bitcast(FP8X4),
+                lhsT_scale=zs[:, c0 : c0 + P],
+                rhs=wq[:, g * CH : (g + 1) * CH].bitcast(FP8X4),
+                rhs_scale=ws[:, g * CH : (g + 1) * CH],
+                start=(g == 0),
+                stop=(g == 1),
+            )
+
+        def p1(s, tl):
+            if tl == 0:
+                st["w", s] = work.tile([P, 2 * CH], F32, tag="w", bufs=LAG + 2, name="w")
+            dst = st["w", s][:, tl * CH : (tl + 1) * CH]
+            if bias_on_pe(s, tl):
+                nc.scalar.copy(out=dst, in_=st["pl", s, tl][:])
+            else:
+                nc.vector.tensor_tensor(out=dst, in0=st["pl", s, tl][:], in1=biasb[:], op=ADD)
+
+        def p2(s, tl):
+            dst = st["w", s][:, tl * CH : (tl + 1) * CH]
+            nc.vector.tensor_tensor(out=dst, in0=st["mx", s, tl][:], in1=dst, op=ADD)
+
+        def p3(s, lo, hi):
+            w = st["w", s][:, lo * CH : hi * CH]
+            nc.scalar.activation(out=w, in_=w, func=SIGMOID)
+
+        def p4(s, lo, hi, eng):
+            bh, j = divmod(s, PER_HALF)
+            w3 = st["w", s][:].rearrange("p (t c) -> p t c", t=2)[:, lo:hi, :]
+            c3 = cel[s][:, lo:hi, :]
+            dst = w3
+            if ACC_MODE == "v" and j == 0:
+                if lo == 0:
+                    st["accp", bh] = work.tile([P, 2 * CH], F32, tag="accp", bufs=2, name="accp")
+                dst = st["accp", bh][:].rearrange("p (t c) -> p t c", t=2)[:, lo:hi, :]
+            eng.tensor_tensor(out=dst, in0=w3, in1=c3, op=MULT)
+
+        def pair_add(s):
+            w = st["w", s]
+            nc.vector.tensor_tensor(out=w[:, 0:CH], in0=w[:, 0:CH], in1=w[:, CH:], op=ADD)
+
+        def summed_tiles(s):
+            return (0,) if (ACC_MODE == "pe2" and s < NPAIR - 1) else (0, 1)
+
+        def acc_t(s, tl, cb):
+            bh, j = divmod(s, PER_HALF)
+            first = j == 0 and tl == 0 and cb == 0
+            if first:
+                st["acc", bh] = bank("acc", 1)
+            nc.tensor.matmul(
+                out=st["acc", bh][:, cb * P : (cb + 1) * P],
+                lhsT=st["w", s][:, tl * CH + cb * P : tl * CH + (cb + 1) * P],
+                rhs=ident[:],
+                is_transpose=True,
+                start=first,
+                stop=((j == PER_HALF - 1 or s == NAT_FROM - 1) and tl == 1 and cb == 3),
+            )
+
+        def p5(s):
+            bh, j = divmod(s, PER_HALF)
+            if j > 0:
+                a = st["accp", bh]
+                nc.vector.tensor_tensor(out=a[:], in0=a[:], in1=st["w", s][:], op=ADD)
+
+        def store(bh, res):
+            nc.sync.dma_start(out=out[bh * P : (bh + 1) * P, :], in_=res[:])
+
+        def ro_copy(bh):
+            accs = work.tile([P, 512], F32, tag="accs", bufs=1, name="accs")
+            nc.scalar.copy(out=accs[:], in_=st["acc", bh][:])
+            st["accs", bh] = accs
+
+        def ro_back(bh, finish):
+            ops = bank("hps", 1)
+            st["ops", bh] = ops
+            for cb in range(4):
+                nc.tensor.transpose(
+                    ops[:, cb * P : (cb + 1) * P], st["accs", bh][:, cb * P : (cb + 1) * P], ident[:]
+                )
+            if finish:
+                res = work.tile([P, CH], F32, tag="res", bufs=2, name="res")
+                nc.scalar.copy(out=res[:], in_=ops[:])
+                store(bh, res)
+
+        def fin_v(bh):
+            a = st["accp", bh]
+            res = work.tile([P, CH], F32, tag="res", bufs=2, name="res")
+            nc.vector.tensor_tensor(out=res[:], in0=a[:, 0:CH], in1=a[:, CH:], op=ADD)
+            store(bh, res)
+
+        def weave(mats, trans):
+            gaps = len(mats) - 1 if TAIL_FREE else len(mats)
+            done = 0
+            for i, m in enumerate(mats):
+                m()
+                upto = min(len(trans), (len(trans) * (i + 1) + gaps - 1) // gaps)
+                while done < upto:
+                    trans[done]()
+                    done += 1
+            while done < len(trans):
+                trans[done]()
+                done += 1
+
+        ut = const.tile([P, 2 * CH], F32, name="ut")
+        for v in range(2):
+            ups = bank("pl", 2)
+            for t in range(4):
+                nc.tensor.transpose(
+                    ups[:, t * P : (t + 1) * P],
+                    un[:].bitcast(F32)[:, t * 256 + v * P : t * 256 + (v + 1) * P],
+                    ident[:],
+                )
+            if v == 0:
+                nc.scalar.copy(out=ut[:, 0:CH], in_=ups[:])
+            else:
+                nc.vector.tensor_copy(out=ut[:, CH:], in_=ups[:])
+        ut16 = ut[:].bitcast(BF16).rearrange("p (v c e) -> p v c e", v=2, e=2)
+
+        for i in range(4):
+            t_h(0, i)
+        c_h(0)
+
+        bps = bank("acc", 1)
+        nc.tensor.matmul(out=bps[:], lhsT=ones[:], rhs=brow[:], start=True, stop=True)
+        biasb = const.tile([P, CH], F32, name="biasb")
+        nc.vector.tensor_copy(out=biasb[:], in_=bps[:])
+
+        wg = const.tile([P, 2 * CH * 4], BF16, name="wg", align_bytes=64)
+        wq = const.tile([P, 2 * CH], U32, name="wq", align_bytes=64)
+        ws = const.tile([P, 2 * CH], U8, name="ws", align_bytes=64)
+
+        def t_w(i):
+            q, r = divmod(i, 4)
+            g, hh = divmod(q, 2)
+            u, t = divmod(r, 2)
+            if r == 0:
+                st["wps", q] = bank(("zps", "mx")[q % 2], 2)
+            nc.tensor.transpose(
+                st["wps", q][:, r * P : (r + 1) * P],
+                wn[:].bitcast(F32)[:, (2 * hh + t) * 512 + g * 256 + u : (2 * hh + t) * 512 + (g + 1) * 256 : 2],
+                ident[:],
+            )
+
+        def c_w():
+            for q in range(4):
+                src = st["wps", q][:].rearrange("p (u x) -> p x u", u=2)
+                dst = wg[:].bitcast(F32)[:, q * 512 : (q + 1) * 512].rearrange("p (x u) -> p x u", u=2)
+                if q % 2 == 0:
+                    nc.scalar.copy(out=dst, in_=src)
+                else:
+                    nc.vector.tensor_copy(out=dst, in_=src)
+            nc.vector.quantize_mx(out=wq[:].bitcast(FP8X4), scales=ws[:], in_=wg[:])
+
+        def half(s, tl):
+            return st["w", s][:, tl * CH : (tl + 1) * CH]
+
+        def add_v(dst, x, y):
+            nc.vector.tensor_tensor(out=dst, in0=x, in1=y, op=ADD)
+
+        LAST = NPAIR - 1
+        for s in range(NPAIR):
+            a = s - LAG
+            m = s - 1
+            mats = []
+            for tl in range(2):
+                for i in range(5 if bias_on_pe(s, tl) else 4):
+                    mats.append(lambda s=s, tl=tl, i=i: mm_plain(s, tl, i))
+            t_hs = [lambda s=s, i=i: t_h(s + 1, i) for i in range(4)] if s < LAST else []
+            t_zs = [lambda s=s, i=i: t_z(s, i) for i in range(8)]
+            accs = [lambda a=a, i=i: acc_t(a, i // 4, i % 4) for i in range(8)] if a >= 0 else []
+            if s == 0:
+                weave(mats[:4], [lambda i=i: t_w(i) for i in range(16)])
+                p1(0, 0)
+                c_w()
+                mats = mats[4:]
+            weave(mats, t_zs + accs if s == LAST else t_hs + accs + t_zs)
+            if s < LAST:
+                c_h(s + 1)
+            c_z(s, 0)
+            c_z(s, 1)
+            if a == PER_HALF:
+                ro_back(0, True)
+            if a == PER_HALF - 1:
+                ro_copy(0)
+            if s > 0:
+                p1(s, 0)
+            if s == LAST:
+                q_z(s)
+            p1(s, 1)
+            if m >= 0:
+                for tl in range(2):
+                    for g in range(2):
+                        mm_mx(m, tl, g)
+            if s < LAST:
+                if m >= 0:
+                    p2(m, 0)
+                    p2(m, 1)
+                q_z(s)
+                if m >= 0:
+                    p3(m, 0, 2)
+                    p4(m, 0, 2, nc.gpsimd)
+
+        p2(LAST - 1, 0)
+        p3(LAST - 1, 0, 1)
+        p4(LAST - 1, 0, 1, nc.gpsimd)
+        p2(LAST - 1, 1)
+        p3(LAST - 1, 1, 2)
+        for tl in range(2):
+            for g in range(2):
+                mm_mx(LAST, tl, g)
+        for tl in range(2):
+            p2(LAST, tl)
+            p3(LAST, tl, tl + 1)
+        p4(LAST - 1, 1, 2, nc.vector)
+        for a in (LAST - 2, LAST - 1):
+            for i in range(8):
+                acc_t(a, i // 4, i % 4)
+        ro_copy(1)
+        ro_back(1, False)
+        p4(LAST, 0, 1, nc.vector)
+        p4(LAST, 1, 2, nc.vector)
+        add_v(half(LAST, 0), half(LAST, 0), half(LAST, 1))
+        res = work.tile([P, CH], F32, tag="res", bufs=2, name="res")
+        add_v(res[:], st["ops", 1][:], half(LAST, 0))
+        store(1, res)

@@ -110,12 +110,21 @@ def tile_treelstm_pa_kernel(tc, z_node, z_children, W_f, U_f, b_f, out):
 
         def t_z(s, i):
             tl, wb = divmod(i, 4)
+            g, u = divmod(wb, 2)
             if wb == 0:
                 st["zps", s, tl] = bank("zps", 2)
-            nc.tensor.transpose(
-                st["zps", s, tl][:, wb * P : (wb + 1) * P],
-                zn[s][:].bitcast(F32)[:, tl * 512 + (wb // 2) * 256 + wb % 2 : tl * 512 + (wb // 2 + 1) * 256 : 2],
-                ident[:],
+            if s == 0:
+                words = zn[s][:].bitcast(F32)[:, tl * 512 + g * 256 + u : tl * 512 + (g + 1) * 256 : 2]
+            else:
+                words = st["sz", s][:, tl * 512 + wb * P : tl * 512 + (wb + 1) * P]
+            nc.tensor.transpose(st["zps", s, tl][:, wb * P : (wb + 1) * P], words, ident[:])
+
+        def sort_z(s, tl):
+            if tl == 0:
+                st["sz", s] = work.tile([P, SIZE], F32, tag="sz", bufs=2, name="sz")
+            nc.scalar.copy(
+                out=st["sz", s][:, tl * 512 : (tl + 1) * 512].rearrange("p (g u r) -> p g u r", g=2, u=2),
+                in_=zn[s][:].bitcast(F32)[:, tl * 512 : (tl + 1) * 512].rearrange("p (g r u) -> p g u r", g=2, u=2),
             )
 
         def c_z(s, tl):
@@ -333,7 +342,10 @@ def tile_treelstm_pa_kernel(tc, z_node, z_children, W_f, U_f, b_f, out):
             weave(mats, t_zs + accs if s == LAST else t_hs + accs + t_zs)
             if s < LAST:
                 c_h(s + 1)
+                sort_z(s + 1, 0)
             c_z(s, 0)
+            if s < LAST:
+                sort_z(s + 1, 1)
             c_z(s, 1)
             if a == PER_HALF:
                 ro_back(0, True)

@@ -16,13 +16,10 @@ P = 128
 B, N, SIZE, CH = 256, 16, 1024, 512
 FLOPS = 2 * B * N * (SIZE + CH) * CH
 
-NPAIR = 16
+PAIRS = 16
 PER_HALF = 8
-ACC_MODE = "pe"
+LAST = PAIRS - 1
 LAG = 3
-BIAS_PE = ()
-TAIL_FREE = True
-NAT_FROM = NPAIR - 1
 
 
 def tile_treelstm_pa_kernel(tc, z_node, z_children, W_f, U_f, b_f, out):
@@ -88,10 +85,10 @@ def tile_treelstm_pa_kernel(tc, z_node, z_children, W_f, U_f, b_f, out):
         hid[1] = load_part(1, 0, "zh")
         cel[0] = load_part(0, CH, "zcc")
         cel[1] = load_part(1, CH, "zcc")
-        for s in range(1, NPAIR):
-            if s + 1 < NPAIR:
-                load_children(s + 1)
+        for s in range(1, PAIRS):
             zn[s] = load_pair(z_node, s, "zn")
+            if s + 1 < PAIRS:
+                load_children(s + 1)
 
         def t_h(s, i):
             if i == 0:
@@ -108,24 +105,23 @@ def tile_treelstm_pa_kernel(tc, z_node, z_children, W_f, U_f, b_f, out):
             nc.scalar.copy(out=ht[:], in_=st["hps", s][:])
             st["ht", s] = ht[:].bitcast(BF16).rearrange("p (t v r e) -> p t v r e", t=2, v=2, e=2)
 
-        def t_z(s, i):
-            tl, wb = divmod(i, 4)
-            g, u = divmod(wb, 2)
-            if wb == 0:
-                st["zps", s, tl] = bank("zps", 2)
-            if s == 0:
-                words = zn[s][:].bitcast(F32)[:, tl * 512 + g * 256 + u : tl * 512 + (g + 1) * 256 : 2]
-            else:
-                words = st["sz", s][:, tl * 512 + wb * P : tl * 512 + (wb + 1) * P]
-            nc.tensor.transpose(st["zps", s, tl][:, wb * P : (wb + 1) * P], words, ident[:])
-
         def sort_z(s, tl):
             if tl == 0:
-                st["sz", s] = work.tile([P, SIZE], F32, tag="sz", bufs=2, name="sz")
+                st["sz", s] = work.tile([P, SIZE], F32, tag="sz", bufs=3, name="sz")
             nc.scalar.copy(
                 out=st["sz", s][:, tl * 512 : (tl + 1) * 512].rearrange("p (g u r) -> p g u r", g=2, u=2),
                 in_=zn[s][:].bitcast(F32)[:, tl * 512 : (tl + 1) * 512].rearrange("p (g r u) -> p g u r", g=2, u=2),
             )
+
+        def t_z(s, tl, i):
+            g, u = divmod(i, 2)
+            if i == 0:
+                st["zps", s, tl] = bank("zps", 2)
+            if s == 0:
+                words = zn[s][:].bitcast(F32)[:, tl * 512 + g * 256 + u : tl * 512 + (g + 1) * 256 : 2]
+            else:
+                words = st["sz", s][:, tl * 512 + i * P : tl * 512 + (i + 1) * P]
+            nc.tensor.transpose(st["zps", s, tl][:, i * P : (i + 1) * P], words, ident[:])
 
         def c_z(s, tl):
             if tl == 0:
@@ -137,96 +133,71 @@ def tile_treelstm_pa_kernel(tc, z_node, z_children, W_f, U_f, b_f, out):
             )
 
         def q_z(s):
-            zq = work.tile([P, 512], U32, tag="zq", bufs=3, name="zq", align_bytes=64)
-            zs = work.tile([P, 512], U8, tag="zs", bufs=3, name="zs", align_bytes=64)
+            zq = work.tile([P, 512], U32, tag="zq", bufs=4, name="zq", align_bytes=64)
+            zs = work.tile([P, 512], U8, tag="zs", bufs=4, name="zs", align_bytes=64)
             nc.vector.quantize_mx(out=zq[:].bitcast(FP8X4), scales=zs[:], in_=st["zg", s][:])
             st["zq", s] = (zq, zs)
-
-        def bias_on_pe(s, tl):
-            return (2 * s + tl) % 8 in BIAS_PE
 
         def mm_plain(s, tl, i):
             if i == 0:
                 st["pl", s, tl] = bank("pl", 2)
-            last = 4 if bias_on_pe(s, tl) else 3
-            if i < 4:
-                v, e = divmod(i, 2)
-                lhs = st["ht", s][:, tl, v, :, e]
-                rhs = ut16[:, v, :, e]
-            else:
-                lhs = ones[:]
-                rhs = brow[:]
-            nc.tensor.matmul(out=st["pl", s, tl][:], lhsT=lhs, rhs=rhs, start=(i == 0), stop=(i == last))
-
-        def mm_mx(s, tl, g):
-            if g == 0:
-                st["mx", s, tl] = bank("mx", 2)
-            zq, zs = st["zq", s]
-            c0 = (tl * 2 + g) * P
-            nc.tensor.matmul_mx(
-                out=st["mx", s, tl][:],
-                lhsT=zq[:, c0 : c0 + P].bitcast(FP8X4),
-                lhsT_scale=zs[:, c0 : c0 + P],
-                rhs=wq[:, g * CH : (g + 1) * CH].bitcast(FP8X4),
-                rhs_scale=ws[:, g * CH : (g + 1) * CH],
-                start=(g == 0),
-                stop=(g == 1),
+            v, e = divmod(i, 2)
+            nc.tensor.matmul(
+                out=st["pl", s, tl][:],
+                lhsT=st["ht", s][:, tl, v, :, e],
+                rhs=ut16[:, v, :, e],
+                start=(i == 0),
+                stop=(i == 3),
             )
+
+        def mm_mx(s, tl):
+            st["mx", s, tl] = bank("mx", 2)
+            zq, zs = st["zq", s]
+            for g in range(2):
+                c0 = (tl * 2 + g) * P
+                nc.tensor.matmul_mx(
+                    out=st["mx", s, tl][:],
+                    lhsT=zq[:, c0 : c0 + P].bitcast(FP8X4),
+                    lhsT_scale=zs[:, c0 : c0 + P],
+                    rhs=wq[:, g * CH : (g + 1) * CH].bitcast(FP8X4),
+                    rhs_scale=ws[:, g * CH : (g + 1) * CH],
+                    start=(g == 0),
+                    stop=(g == 1),
+                )
+
+        def half(s, tl):
+            return st["w", s][:, tl * CH : (tl + 1) * CH]
 
         def p1(s, tl):
             if tl == 0:
                 st["w", s] = work.tile([P, 2 * CH], F32, tag="w", bufs=LAG + 2, name="w")
-            dst = st["w", s][:, tl * CH : (tl + 1) * CH]
-            if bias_on_pe(s, tl):
-                nc.scalar.copy(out=dst, in_=st["pl", s, tl][:])
-            else:
-                nc.vector.tensor_tensor(out=dst, in0=st["pl", s, tl][:], in1=biasb[:], op=ADD)
+            nc.vector.tensor_tensor(out=half(s, tl), in0=st["pl", s, tl][:], in1=biasb[:], op=ADD)
 
         def p2(s, tl):
-            dst = st["w", s][:, tl * CH : (tl + 1) * CH]
-            nc.vector.tensor_tensor(out=dst, in0=st["mx", s, tl][:], in1=dst, op=ADD)
+            nc.vector.tensor_tensor(out=half(s, tl), in0=st["mx", s, tl][:], in1=half(s, tl), op=ADD)
 
         def p3(s, lo, hi):
             w = st["w", s][:, lo * CH : hi * CH]
             nc.scalar.activation(out=w, in_=w, func=SIGMOID)
 
         def p4(s, lo, hi, eng):
-            bh, j = divmod(s, PER_HALF)
             w3 = st["w", s][:].rearrange("p (t c) -> p t c", t=2)[:, lo:hi, :]
-            c3 = cel[s][:, lo:hi, :]
-            dst = w3
-            if ACC_MODE == "v" and j == 0:
-                if lo == 0:
-                    st["accp", bh] = work.tile([P, 2 * CH], F32, tag="accp", bufs=2, name="accp")
-                dst = st["accp", bh][:].rearrange("p (t c) -> p t c", t=2)[:, lo:hi, :]
-            eng.tensor_tensor(out=dst, in0=w3, in1=c3, op=MULT)
+            eng.tensor_tensor(out=w3, in0=w3, in1=cel[s][:, lo:hi, :], op=MULT)
 
-        def pair_add(s):
-            w = st["w", s]
-            nc.vector.tensor_tensor(out=w[:, 0:CH], in0=w[:, 0:CH], in1=w[:, CH:], op=ADD)
-
-        def summed_tiles(s):
-            return (0,) if (ACC_MODE == "pe2" and s < NPAIR - 1) else (0, 1)
-
-        def acc_t(s, tl, cb):
+        def acc_t(s, i):
             bh, j = divmod(s, PER_HALF)
-            first = j == 0 and tl == 0 and cb == 0
+            tl, cb = divmod(i, 4)
+            first = j == 0 and i == 0
             if first:
                 st["acc", bh] = bank("acc", 1)
             nc.tensor.matmul(
                 out=st["acc", bh][:, cb * P : (cb + 1) * P],
-                lhsT=st["w", s][:, tl * CH + cb * P : tl * CH + (cb + 1) * P],
+                lhsT=st["w", s][:, i * P : (i + 1) * P],
                 rhs=ident[:],
                 is_transpose=True,
                 start=first,
-                stop=((j == PER_HALF - 1 or s == NAT_FROM - 1) and tl == 1 and cb == 3),
+                stop=((j == PER_HALF - 1 or s == LAST - 1) and i == 7),
             )
-
-        def p5(s):
-            bh, j = divmod(s, PER_HALF)
-            if j > 0:
-                a = st["accp", bh]
-                nc.vector.tensor_tensor(out=a[:], in0=a[:], in1=st["w", s][:], op=ADD)
 
         def store(bh, res):
             nc.sync.dma_start(out=out[bh * P : (bh + 1) * P, :], in_=res[:])
@@ -236,26 +207,22 @@ def tile_treelstm_pa_kernel(tc, z_node, z_children, W_f, U_f, b_f, out):
             nc.scalar.copy(out=accs[:], in_=st["acc", bh][:])
             st["accs", bh] = accs
 
-        def ro_back(bh, finish):
+        def ro_back(bh):
             ops = bank("hps", 1)
             st["ops", bh] = ops
             for cb in range(4):
                 nc.tensor.transpose(
                     ops[:, cb * P : (cb + 1) * P], st["accs", bh][:, cb * P : (cb + 1) * P], ident[:]
                 )
-            if finish:
-                res = work.tile([P, CH], F32, tag="res", bufs=2, name="res")
-                nc.scalar.copy(out=res[:], in_=ops[:])
-                store(bh, res)
 
-        def fin_v(bh):
-            a = st["accp", bh]
-            res = work.tile([P, CH], F32, tag="res", bufs=2, name="res")
-            nc.vector.tensor_tensor(out=res[:], in0=a[:, 0:CH], in1=a[:, CH:], op=ADD)
-            store(bh, res)
+        def new_res():
+            return work.tile([P, CH], F32, tag="res", bufs=2, name="res")
+
+        def add_v(dst, x, y):
+            nc.vector.tensor_tensor(out=dst, in0=x, in1=y, op=ADD)
 
         def weave(mats, trans):
-            gaps = len(mats) - 1 if TAIL_FREE else len(mats)
+            gaps = len(mats) - 1
             done = 0
             for i, m in enumerate(mats):
                 m()
@@ -263,9 +230,13 @@ def tile_treelstm_pa_kernel(tc, z_node, z_children, W_f, U_f, b_f, out):
                 while done < upto:
                     trans[done]()
                     done += 1
-            while done < len(trans):
-                trans[done]()
-                done += 1
+
+        def turn(steps, copy):
+            def last():
+                steps[-1]()
+                copy()
+
+            return steps[:-1] + [last]
 
         ut = const.tile([P, 2 * CH], F32, name="ut")
         for v in range(2):
@@ -286,11 +257,6 @@ def tile_treelstm_pa_kernel(tc, z_node, z_children, W_f, U_f, b_f, out):
             t_h(0, i)
         c_h(0)
 
-        bps = bank("acc", 1)
-        nc.tensor.matmul(out=bps[:], lhsT=ones[:], rhs=brow[:], start=True, stop=True)
-        biasb = const.tile([P, CH], F32, name="biasb")
-        nc.vector.tensor_copy(out=biasb[:], in_=bps[:])
-
         wg = const.tile([P, 2 * CH * 4], BF16, name="wg", align_bytes=64)
         wq = const.tile([P, 2 * CH], U32, name="wq", align_bytes=64)
         ws = const.tile([P, 2 * CH], U8, name="ws", align_bytes=64)
@@ -307,88 +273,93 @@ def tile_treelstm_pa_kernel(tc, z_node, z_children, W_f, U_f, b_f, out):
                 ident[:],
             )
 
-        def c_w():
-            for q in range(4):
-                src = st["wps", q][:].rearrange("p (u x) -> p x u", u=2)
-                dst = wg[:].bitcast(F32)[:, q * 512 : (q + 1) * 512].rearrange("p (x u) -> p x u", u=2)
-                if q % 2 == 0:
-                    nc.scalar.copy(out=dst, in_=src)
-                else:
-                    nc.vector.tensor_copy(out=dst, in_=src)
-            nc.vector.quantize_mx(out=wq[:].bitcast(FP8X4), scales=ws[:], in_=wg[:])
+        def c_w(q):
+            src = st["wps", q][:].rearrange("p (u x) -> p x u", u=2)
+            dst = wg[:].bitcast(F32)[:, q * 512 : (q + 1) * 512].rearrange("p (x u) -> p x u", u=2)
+            if q % 2 == 0:
+                nc.scalar.copy(out=dst, in_=src)
+            else:
+                nc.vector.tensor_copy(out=dst, in_=src)
 
-        def half(s, tl):
-            return st["w", s][:, tl * CH : (tl + 1) * CH]
+        def mats_of(s, tl):
+            return [lambda i=i: mm_plain(s, tl, i) for i in range(4)]
 
-        def add_v(dst, x, y):
-            nc.vector.tensor_tensor(out=dst, in0=x, in1=y, op=ADD)
+        def accs_of(s):
+            return [lambda i=i: acc_t(s, i) for i in range(8)] if s >= 0 else []
 
-        LAST = NPAIR - 1
-        for s in range(NPAIR):
+        weave(mats_of(0, 0), [lambda i=i: t_w(i) for i in range(16)])
+        bps = bank("acc", 1)
+        nc.tensor.matmul(out=bps[:], lhsT=ones[:], rhs=brow[:], start=True, stop=True)
+        biasb = const.tile([P, CH], F32, name="biasb")
+        nc.vector.tensor_copy(out=biasb[:], in_=bps[:])
+        p1(0, 0)
+        for q in range(4):
+            c_w(q)
+        nc.vector.quantize_mx(out=wq[:].bitcast(FP8X4), scales=ws[:], in_=wg[:])
+
+        def z_of(s):
+            return {0: [0], 1: [1], 2: [2, 3]}.get(s, [s + 1] if s < LAST else [])
+
+        for s in range(LAST):
             a = s - LAG
             m = s - 1
-            mats = []
-            for tl in range(2):
-                for i in range(5 if bias_on_pe(s, tl) else 4):
-                    mats.append(lambda s=s, tl=tl, i=i: mm_plain(s, tl, i))
-            t_hs = [lambda s=s, i=i: t_h(s + 1, i) for i in range(4)] if s < LAST else []
-            t_zs = [lambda s=s, i=i: t_z(s, i) for i in range(8)]
-            accs = [lambda a=a, i=i: acc_t(a, i // 4, i % 4) for i in range(8)] if a >= 0 else []
-            if s == 0:
-                weave(mats[:4], [lambda i=i: t_w(i) for i in range(16)])
-                p1(0, 0)
-                c_w()
-                mats = mats[4:]
-            weave(mats, t_zs + accs if s == LAST else t_hs + accs + t_zs)
-            if s < LAST:
-                c_h(s + 1)
-                sort_z(s + 1, 0)
-            c_z(s, 0)
-            if s < LAST:
-                sort_z(s + 1, 1)
-            c_z(s, 1)
+            steps = turn([lambda i=i: t_h(s + 1, i) for i in range(4)], lambda: c_h(s + 1)) + accs_of(a)
+            for z in z_of(s):
+                for tl in range(2):
+                    steps += turn(
+                        [lambda z=z, tl=tl, i=i: t_z(z, tl, i) for i in range(4)], lambda z=z, tl=tl: c_z(z, tl)
+                    )
+                    if tl == 1 and z != z_of(s)[-1]:
+                        steps.append(lambda z=z: q_z(z))
+            weave((mats_of(s, 0) if s > 0 else []) + mats_of(s, 1), steps)
             if a == PER_HALF:
-                ro_back(0, True)
+                ro_back(0)
+                res = new_res()
+                nc.scalar.copy(out=res[:], in_=st["ops", 0][:])
+                store(0, res)
             if a == PER_HALF - 1:
                 ro_copy(0)
             if s > 0:
                 p1(s, 0)
-            if s == LAST:
-                q_z(s)
             p1(s, 1)
             if m >= 0:
                 for tl in range(2):
-                    for g in range(2):
-                        mm_mx(m, tl, g)
-            if s < LAST:
-                if m >= 0:
-                    p2(m, 0)
-                    p2(m, 1)
-                q_z(s)
-                if m >= 0:
-                    p3(m, 0, 2)
-                    p4(m, 0, 2, nc.gpsimd)
+                    mm_mx(m, tl)
+                p2(m, 0)
+                p2(m, 1)
+            q_z(z_of(s)[-1])
+            for z in z_of(s + 1):
+                sort_z(z, 0)
+                sort_z(z, 1)
+            if m >= 0:
+                p3(m, 0, 2)
+                p4(m, 0, 2, nc.gpsimd)
 
-        p2(LAST - 1, 0)
-        p3(LAST - 1, 0, 1)
+        mm_mx(LAST - 1, 0)
+        mm_mx(LAST - 1, 1)
+        weave(mats_of(LAST, 0), accs_of(LAST - LAG))
+        for tl in range(2):
+            p2(LAST - 1, tl)
+            p3(LAST - 1, tl, tl + 1)
         p4(LAST - 1, 0, 1, nc.gpsimd)
-        p2(LAST - 1, 1)
-        p3(LAST - 1, 1, 2)
-        for tl in range(2):
-            for g in range(2):
-                mm_mx(LAST, tl, g)
-        for tl in range(2):
-            p2(LAST, tl)
-            p3(LAST, tl, tl + 1)
+        p1(LAST, 0)
+        mm_mx(LAST, 0)
         p4(LAST - 1, 1, 2, nc.vector)
-        for a in (LAST - 2, LAST - 1):
-            for i in range(8):
-                acc_t(a, i // 4, i % 4)
+        p2(LAST, 0)
+        p3(LAST, 0, 1)
+        for mat in mats_of(LAST, 1):
+            mat()
+        p1(LAST, 1)
+        mm_mx(LAST, 1)
+        p2(LAST, 1)
+        p3(LAST, 1, 2)
+        for acc in accs_of(LAST - 2) + accs_of(LAST - 1):
+            acc()
         ro_copy(1)
-        ro_back(1, False)
+        ro_back(1)
         p4(LAST, 0, 1, nc.vector)
         p4(LAST, 1, 2, nc.vector)
         add_v(half(LAST, 0), half(LAST, 0), half(LAST, 1))
-        res = work.tile([P, CH], F32, tag="res", bufs=2, name="res")
+        res = new_res()
         add_v(res[:], st["ops", 1][:], half(LAST, 0))
         store(1, res)

@@ -19,7 +19,9 @@ FLOPS = 2 * B * N * (SIZE + CH) * CH
 PAIRS = 16
 PER_HALF = 8
 LAST = PAIRS - 1
-LAG = 3
+UNSORTED = 3
+LATE = 12
+LAG = 4
 
 
 def tile_treelstm_pa_kernel(tc, z_node, z_children, W_f, U_f, b_f, out):
@@ -105,19 +107,19 @@ def tile_treelstm_pa_kernel(tc, z_node, z_children, W_f, U_f, b_f, out):
             nc.scalar.copy(out=ht[:], in_=st["hps", s][:])
             st["ht", s] = ht[:].bitcast(BF16).rearrange("p (t v r e) -> p t v r e", t=2, v=2, e=2)
 
-        def sort_z(s, tl):
-            if tl == 0:
-                st["sz", s] = work.tile([P, SIZE], F32, tag="sz", bufs=3, name="sz")
-            nc.scalar.copy(
-                out=st["sz", s][:, tl * 512 : (tl + 1) * 512].rearrange("p (g u r) -> p g u r", g=2, u=2),
-                in_=zn[s][:].bitcast(F32)[:, tl * 512 : (tl + 1) * 512].rearrange("p (g r u) -> p g u r", g=2, u=2),
+        def sort_z(s):
+            sz = work.tile([P, SIZE], F32, tag="sz", bufs=4, name="sz")
+            nc.vector.tensor_copy(
+                out=sz[:].rearrange("p (q u r) -> p q u r", q=4, u=2),
+                in_=zn[s][:].bitcast(F32).rearrange("p (q r u) -> p q u r", q=4, u=2),
             )
+            st["sz", s] = sz
 
         def t_z(s, tl, i):
             g, u = divmod(i, 2)
             if i == 0:
                 st["zps", s, tl] = bank("zps", 2)
-            if s == 0:
+            if s < UNSORTED:
                 words = zn[s][:].bitcast(F32)[:, tl * 512 + g * 256 + u : tl * 512 + (g + 1) * 256 : 2]
             else:
                 words = st["sz", s][:, tl * 512 + i * P : tl * 512 + (i + 1) * P]
@@ -184,19 +186,21 @@ def tile_treelstm_pa_kernel(tc, z_node, z_children, W_f, U_f, b_f, out):
             w3 = st["w", s][:].rearrange("p (t c) -> p t c", t=2)[:, lo:hi, :]
             eng.tensor_tensor(out=w3, in0=w3, in1=cel[s][:, lo:hi, :], op=MULT)
 
+        def pair_sum(s):
+            nc.vector.tensor_tensor(out=half(s, 0), in0=half(s, 0), in1=half(s, 1), op=ADD)
+
         def acc_t(s, i):
             bh, j = divmod(s, PER_HALF)
-            tl, cb = divmod(i, 4)
             first = j == 0 and i == 0
             if first:
                 st["acc", bh] = bank("acc", 1)
             nc.tensor.matmul(
-                out=st["acc", bh][:, cb * P : (cb + 1) * P],
+                out=st["acc", bh][:, i % 4 * P : (i % 4 + 1) * P],
                 lhsT=st["w", s][:, i * P : (i + 1) * P],
                 rhs=ident[:],
                 is_transpose=True,
                 start=first,
-                stop=((j == PER_HALF - 1 or s == LAST - 1) and i == 7),
+                stop=((s, i) in ((PER_HALF - 1, 3), (LAST - 1, 7))),
             )
 
         def store(bh, res):
@@ -285,7 +289,7 @@ def tile_treelstm_pa_kernel(tc, z_node, z_children, W_f, U_f, b_f, out):
             return [lambda i=i: mm_plain(s, tl, i) for i in range(4)]
 
         def accs_of(s):
-            return [lambda i=i: acc_t(s, i) for i in range(8)] if s >= 0 else []
+            return [lambda i=i: acc_t(s, i) for i in range(4 if s < LAST - 2 else 8)] if s >= 0 else []
 
         weave(mats_of(0, 0), [lambda i=i: t_w(i) for i in range(16)])
         bps = bank("acc", 1)
@@ -295,22 +299,27 @@ def tile_treelstm_pa_kernel(tc, z_node, z_children, W_f, U_f, b_f, out):
         p1(0, 0)
         for q in range(4):
             c_w(q)
-        nc.vector.quantize_mx(out=wq[:].bitcast(FP8X4), scales=ws[:], in_=wg[:])
 
-        def z_of(s):
-            return {0: [0], 1: [1], 2: [2, 3]}.get(s, [s + 1] if s < LAST else [])
+        def tiles_of(s):
+            lo = 2 * s + (s > LATE) + (s > LATE + 1)
+            hi = 2 * s + 2 + (s >= LATE) + (s >= LATE + 1)
+            return range(lo, hi) if s < LAST else []
+
+        def whole(s):
+            return [t // 2 for t in tiles_of(s) if t % 2 == 1]
+
+        def sorts_of(s):
+            return [t // 2 for t in tiles_of(s + 2) if t % 2 == 0 and t // 2 >= UNSORTED]
 
         for s in range(LAST):
             a = s - LAG
             m = s - 1
             steps = turn([lambda i=i: t_h(s + 1, i) for i in range(4)], lambda: c_h(s + 1)) + accs_of(a)
-            for z in z_of(s):
-                for tl in range(2):
-                    steps += turn(
-                        [lambda z=z, tl=tl, i=i: t_z(z, tl, i) for i in range(4)], lambda z=z, tl=tl: c_z(z, tl)
-                    )
-                    if tl == 1 and z != z_of(s)[-1]:
-                        steps.append(lambda z=z: q_z(z))
+            for t in tiles_of(s):
+                z, tl = divmod(t, 2)
+                steps += turn(
+                    [lambda z=z, tl=tl, i=i: t_z(z, tl, i) for i in range(4)], lambda z=z, tl=tl: c_z(z, tl)
+                )
             weave((mats_of(s, 0) if s > 0 else []) + mats_of(s, 1), steps)
             if a == PER_HALF:
                 ro_back(0)
@@ -327,10 +336,14 @@ def tile_treelstm_pa_kernel(tc, z_node, z_children, W_f, U_f, b_f, out):
                     mm_mx(m, tl)
                 p2(m, 0)
                 p2(m, 1)
-            q_z(z_of(s)[-1])
-            for z in z_of(s + 1):
-                sort_z(z, 0)
-                sort_z(z, 1)
+            if s == 0:
+                nc.vector.quantize_mx(out=wq[:].bitcast(FP8X4), scales=ws[:], in_=wg[:])
+            for z in whole(s):
+                q_z(z)
+            for z in sorts_of(s):
+                sort_z(z)
+            if s >= 2:
+                pair_sum(s - 2)
             if m >= 0:
                 p3(m, 0, 2)
                 p4(m, 0, 2, nc.gpsimd)
@@ -353,13 +366,13 @@ def tile_treelstm_pa_kernel(tc, z_node, z_children, W_f, U_f, b_f, out):
         mm_mx(LAST, 1)
         p2(LAST, 1)
         p3(LAST, 1, 2)
-        for acc in accs_of(LAST - 2) + accs_of(LAST - 1):
+        for acc in accs_of(LAST - 3) + accs_of(LAST - 2) + accs_of(LAST - 1):
             acc()
         ro_copy(1)
         ro_back(1)
         p4(LAST, 0, 1, nc.vector)
         p4(LAST, 1, 2, nc.vector)
-        add_v(half(LAST, 0), half(LAST, 0), half(LAST, 1))
+        pair_sum(LAST)
         res = new_res()
         add_v(res[:], st["ops", 1][:], half(LAST, 0))
         store(1, res)

@@ -19,8 +19,9 @@ FLOPS = 2 * B * N * (SIZE + CH) * CH
 PAIRS = 16
 PER_HALF = 8
 LAST = PAIRS - 1
-UNSORTED = 3
-LATE = 12
+UNSORTED = 1
+EARLY = 3
+THIRD = (1, 1)
 LAG = 4
 
 
@@ -85,10 +86,10 @@ def tile_treelstm_pa_kernel(tc, z_node, z_children, W_f, U_f, b_f, out):
         )
         zn[0] = load_pair(z_node, 0, "zn")
         hid[1] = load_part(1, 0, "zh")
-        cel[0] = load_part(0, CH, "zcc")
-        cel[1] = load_part(1, CH, "zcc")
         for s in range(1, PAIRS):
             zn[s] = load_pair(z_node, s, "zn")
+            if s < 3:
+                cel[s - 1] = load_part(s - 1, CH, "zcc")
             if s + 1 < PAIRS:
                 load_children(s + 1)
 
@@ -107,12 +108,20 @@ def tile_treelstm_pa_kernel(tc, z_node, z_children, W_f, U_f, b_f, out):
             nc.scalar.copy(out=ht[:], in_=st["hps", s][:])
             st["ht", s] = ht[:].bitcast(BF16).rearrange("p (t v r e) -> p t v r e", t=2, v=2, e=2)
 
+        def sort_words(eng_copy, dst, src):
+            eng_copy(
+                out=dst.rearrange("p (q u r) -> p q u r", u=2, r=P), in_=src.rearrange("p (q r u) -> p q u r", u=2, r=P)
+            )
+
         def sort_z(s):
             sz = work.tile([P, SIZE], F32, tag="sz", bufs=4, name="sz")
-            nc.vector.tensor_copy(
-                out=sz[:].rearrange("p (q u r) -> p q u r", q=4, u=2),
-                in_=zn[s][:].bitcast(F32).rearrange("p (q r u) -> p q u r", q=4, u=2),
-            )
+            words = zn[s][:].bitcast(F32)
+            if s < EARLY:
+                sort_words(nc.vector.tensor_copy, sz[:], words)
+            else:
+                for tl in range(2):
+                    x = slice(tl * 512, (tl + 1) * 512)
+                    sort_words(nc.scalar.copy, sz[:, x], words[:, x])
             st["sz", s] = sz
 
         def t_z(s, tl, i):
@@ -144,16 +153,13 @@ def tile_treelstm_pa_kernel(tc, z_node, z_children, W_f, U_f, b_f, out):
             if i == 0:
                 st["pl", s, tl] = bank("pl", 2)
             v, e = divmod(i, 2)
+            ops = (st["ht", s][:, tl, v, :, e], ut16[:, v, :, e]) if i < 4 else (ones[:], brow[:])
             nc.tensor.matmul(
-                out=st["pl", s, tl][:],
-                lhsT=st["ht", s][:, tl, v, :, e],
-                rhs=ut16[:, v, :, e],
-                start=(i == 0),
-                stop=(i == 3),
+                out=st["pl", s, tl][:], lhsT=ops[0], rhs=ops[1], start=(i == 0), stop=(i == (4 if s == LAST else 3))
             )
 
-        def mm_mx(s, tl):
-            st["mx", s, tl] = bank("mx", 2)
+        def mm_mx(s, tl, tag="mx"):
+            st["mx", s, tl] = bank(tag, 2)
             zq, zs = st["zq", s]
             for g in range(2):
                 c0 = (tl * 2 + g) * P
@@ -261,6 +267,11 @@ def tile_treelstm_pa_kernel(tc, z_node, z_children, W_f, U_f, b_f, out):
             t_h(0, i)
         c_h(0)
 
+        bps = bank("acc", 1)
+        nc.tensor.matmul(out=bps[:], lhsT=ones[:], rhs=brow[:], start=True, stop=True)
+        biasb = const.tile([P, CH], F32, name="biasb")
+        nc.vector.tensor_copy(out=biasb[:], in_=bps[:])
+
         wg = const.tile([P, 2 * CH * 4], BF16, name="wg", align_bytes=64)
         wq = const.tile([P, 2 * CH], U32, name="wq", align_bytes=64)
         ws = const.tile([P, 2 * CH], U8, name="ws", align_bytes=64)
@@ -271,11 +282,8 @@ def tile_treelstm_pa_kernel(tc, z_node, z_children, W_f, U_f, b_f, out):
             u, t = divmod(r, 2)
             if r == 0:
                 st["wps", q] = bank(("zps", "mx")[q % 2], 2)
-            nc.tensor.transpose(
-                st["wps", q][:, r * P : (r + 1) * P],
-                wn[:].bitcast(F32)[:, (2 * hh + t) * 512 + g * 256 + u : (2 * hh + t) * 512 + (g + 1) * 256 : 2],
-                ident[:],
-            )
+            c0 = (2 * hh + t) * 512 + (2 * g + u) * P
+            nc.tensor.transpose(st["wps", q][:, r * P : (r + 1) * P], wsort[:, c0 : c0 + P], ident[:])
 
         def c_w(q):
             src = st["wps", q][:].rearrange("p (u x) -> p x u", u=2)
@@ -285,31 +293,35 @@ def tile_treelstm_pa_kernel(tc, z_node, z_children, W_f, U_f, b_f, out):
             else:
                 nc.vector.tensor_copy(out=dst, in_=src)
 
+        wsort = const.tile([P, 4 * 512], F32, name="wsort")
+        for t in range(4):
+            x = slice(t * 512, (t + 1) * 512)
+            sort_words(nc.vector.tensor_copy, wsort[:, x], wn[:].bitcast(F32)[:, x])
+        sort_z(1)
+
         def mats_of(s, tl):
-            return [lambda i=i: mm_plain(s, tl, i) for i in range(4)]
+            return [lambda i=i: mm_plain(s, tl, i) for i in range(5 if s == LAST else 4)]
 
         def accs_of(s):
             return [lambda i=i: acc_t(s, i) for i in range(4 if s < LAST - 2 else 8)] if s >= 0 else []
 
-        weave(mats_of(0, 0), [lambda i=i: t_w(i) for i in range(16)])
-        bps = bank("acc", 1)
-        nc.tensor.matmul(out=bps[:], lhsT=ones[:], rhs=brow[:], start=True, stop=True)
-        biasb = const.tile([P, CH], F32, name="biasb")
-        nc.vector.tensor_copy(out=biasb[:], in_=bps[:])
+        for mat in mats_of(0, 0):
+            mat()
+        weave(mats_of(0, 1), [lambda i=i: t_w(i) for i in range(16)])
         p1(0, 0)
         for q in range(4):
             c_w(q)
 
         def tiles_of(s):
-            lo = 2 * s + (s > LATE) + (s > LATE + 1)
-            hi = 2 * s + 2 + (s >= LATE) + (s >= LATE + 1)
-            return range(lo, hi) if s < LAST else []
+            lo = 2 * s + sum([1 for x in THIRD if x < s])
+            hi = 2 * s + 2 + sum([1 for x in THIRD if x <= s])
+            return range(lo, min(hi, 2 * PAIRS)) if s < LAST else []
 
         def whole(s):
             return [t // 2 for t in tiles_of(s) if t % 2 == 1]
 
         def sorts_of(s):
-            return [t // 2 for t in tiles_of(s + 2) if t % 2 == 0 and t // 2 >= UNSORTED]
+            return [t // 2 for t in tiles_of(s + 1) if t % 2 == 0 and t // 2 >= EARLY]
 
         for s in range(LAST):
             a = s - LAG
@@ -320,7 +332,11 @@ def tile_treelstm_pa_kernel(tc, z_node, z_children, W_f, U_f, b_f, out):
                 steps += turn(
                     [lambda z=z, tl=tl, i=i: t_z(z, tl, i) for i in range(4)], lambda z=z, tl=tl: c_z(z, tl)
                 )
-            weave((mats_of(s, 0) if s > 0 else []) + mats_of(s, 1), steps)
+            if s == 0:
+                for step in steps:
+                    step()
+            else:
+                weave(mats_of(s, 0) + mats_of(s, 1), steps)
             if a == PER_HALF:
                 ro_back(0)
                 res = new_res()
@@ -337,6 +353,7 @@ def tile_treelstm_pa_kernel(tc, z_node, z_children, W_f, U_f, b_f, out):
                 p2(m, 0)
                 p2(m, 1)
             if s == 0:
+                sort_z(2)
                 nc.vector.quantize_mx(out=wq[:].bitcast(FP8X4), scales=ws[:], in_=wg[:])
             for z in whole(s):
                 q_z(z)
@@ -348,31 +365,40 @@ def tile_treelstm_pa_kernel(tc, z_node, z_children, W_f, U_f, b_f, out):
                 p3(m, 0, 2)
                 p4(m, 0, 2, nc.gpsimd)
 
-        mm_mx(LAST - 1, 0)
-        mm_mx(LAST - 1, 1)
+        mm_mx(LAST - 1, 0, "zps")
+        mm_mx(LAST - 1, 1, "zps")
         weave(mats_of(LAST, 0), accs_of(LAST - LAG))
-        for tl in range(2):
-            p2(LAST - 1, tl)
-            p3(LAST - 1, tl, tl + 1)
-        p4(LAST - 1, 0, 1, nc.gpsimd)
-        p1(LAST, 0)
         mm_mx(LAST, 0)
-        p4(LAST - 1, 1, 2, nc.vector)
-        p2(LAST, 0)
-        p3(LAST, 0, 1)
+        mm_mx(LAST, 1)
         for mat in mats_of(LAST, 1):
             mat()
-        p1(LAST, 1)
-        mm_mx(LAST, 1)
-        p2(LAST, 1)
-        p3(LAST, 1, 2)
+        p2(LAST - 1, 0)
+        p2(LAST - 1, 1)
+        st["w", LAST] = work.tile([P, 2 * CH], F32, tag="w", bufs=LAG + 2, name="w")
+        nc.scalar.copy(out=st["w", LAST][:, 0:CH], in_=st["pl", LAST, 0][:])
+        p3(LAST - 1, 0, 1)
+        p3(LAST - 1, 1, 2)
+        p2(LAST, 0)
+        p3(LAST, 0, 1)
+        p4(LAST - 1, 0, 1, nc.vector)
+        p4(LAST - 1, 1, 2, nc.vector)
+        nc.scalar.copy(out=half(LAST, 1), in_=st["mx", LAST, 1][:])
+        p4(LAST, 0, 1, nc.gpsimd)
         for acc in accs_of(LAST - 3) + accs_of(LAST - 2) + accs_of(LAST - 1):
             acc()
-        ro_copy(1)
+        w = half(LAST, 1)
+        parts = [slice(0, CH // 2), slice(CH // 2, CH)]
+        for x in parts:
+            nc.vector.tensor_tensor(out=w[:, x], in0=st["pl", LAST, 1][:, x], in1=w[:, x], op=ADD)
+            nc.scalar.activation(out=w[:, x], in_=w[:, x], func=SIGMOID)
+        accs = work.tile([P, CH], F32, tag="accs", bufs=1, name="accs")
+        nc.vector.tensor_copy(out=accs[:], in_=st["acc", 1][:])
+        st["accs", 1] = accs
         ro_back(1)
-        p4(LAST, 0, 1, nc.vector)
-        p4(LAST, 1, 2, nc.vector)
-        pair_sum(LAST)
         res = new_res()
         add_v(res[:], st["ops", 1][:], half(LAST, 0))
-        store(1, res)
+        for x in parts:
+            nc.vector.tensor_tensor(out=w[:, x], in0=w[:, x], in1=cel[LAST][:, 1, x], op=MULT)
+        for x in parts:
+            add_v(res[:, x], res[:, x], w[:, x])
+            nc.sync.dma_start(out=out[P : 2 * P, x], in_=res[:, x])

@@ -114,7 +114,7 @@ def tile_treelstm_pa_kernel(tc, z_node, z_children, W_f, U_f, b_f, out):
             )
 
         def sort_z(s):
-            sz = work.tile([P, SIZE], F32, tag="sz", bufs=4, name="sz")
+            sz = work.tile([P, SIZE], F32, tag="sz", bufs=3, name="sz")
             words = zn[s][:].bitcast(F32)
             if s < EARLY:
                 sort_words(nc.vector.tensor_copy, sz[:], words)
@@ -362,8 +362,11 @@ def tile_treelstm_pa_kernel(tc, z_node, z_children, W_f, U_f, b_f, out):
             if s >= 2:
                 pair_sum(s - 2)
             if m >= 0:
-                p3(m, 0, 2)
-                p4(m, 0, 2, nc.gpsimd)
+                p3(m, 0, 1)
+                p4(m, 0, 1, nc.gpsimd)
+                p3(m, 1, 2)
+                if s < LAST - 1:
+                    p4(m, 1, 2, nc.gpsimd)
 
         mm_mx(LAST - 1, 0, "zps")
         mm_mx(LAST - 1, 1, "zps")
@@ -378,12 +381,12 @@ def tile_treelstm_pa_kernel(tc, z_node, z_children, W_f, U_f, b_f, out):
         nc.scalar.copy(out=st["w", LAST][:, 0:CH], in_=st["pl", LAST, 0][:])
         p3(LAST - 1, 0, 1)
         p3(LAST - 1, 1, 2)
+        nc.scalar.copy(out=half(LAST, 1), in_=st["mx", LAST, 1][:])
+        p4(LAST - 2, 1, 2, nc.vector)
         p2(LAST, 0)
         p3(LAST, 0, 1)
         p4(LAST - 1, 0, 1, nc.vector)
         p4(LAST - 1, 1, 2, nc.vector)
-        nc.scalar.copy(out=half(LAST, 1), in_=st["mx", LAST, 1][:])
-        p4(LAST, 0, 1, nc.gpsimd)
         for acc in accs_of(LAST - 3) + accs_of(LAST - 2) + accs_of(LAST - 1):
             acc()
         w = half(LAST, 1)
@@ -391,14 +394,14 @@ def tile_treelstm_pa_kernel(tc, z_node, z_children, W_f, U_f, b_f, out):
         for x in parts:
             nc.vector.tensor_tensor(out=w[:, x], in0=st["pl", LAST, 1][:, x], in1=w[:, x], op=ADD)
             nc.scalar.activation(out=w[:, x], in_=w[:, x], func=SIGMOID)
-        accs = work.tile([P, CH], F32, tag="accs", bufs=1, name="accs")
-        nc.vector.tensor_copy(out=accs[:], in_=st["acc", 1][:])
-        st["accs", 1] = accs
+        p4(LAST, 0, 1, nc.vector)
+        ro_copy(1)
         ro_back(1)
-        res = new_res()
-        add_v(res[:], st["ops", 1][:], half(LAST, 0))
         for x in parts:
             nc.vector.tensor_tensor(out=w[:, x], in0=w[:, x], in1=cel[LAST][:, 1, x], op=MULT)
         for x in parts:
-            add_v(res[:, x], res[:, x], w[:, x])
+            add_v(w[:, x], w[:, x], half(LAST, 0)[:, x])
+        res = new_res()
+        for x in parts:
+            add_v(res[:, x], st["ops", 1][:, x], w[:, x])
             nc.sync.dma_start(out=out[P : 2 * P, x], in_=res[:, x])

@@ -19,6 +19,7 @@ FLOPS = 2 * B * N * (SIZE + CH) * CH
 PAIRS = 16
 PER_HALF = 8
 LAST = PAIRS - 1
+FIRST = 3
 UNSORTED = 1
 EARLY = 3
 THIRD = (1, 1)
@@ -85,13 +86,14 @@ def tile_treelstm_pa_kernel(tc, z_node, z_children, W_f, U_f, b_f, out):
             out=wn[:].rearrange("p (t k) -> p t k", t=4), in_=W_f.rearrange("(t p) k -> p t k", p=P)
         )
         zn[0] = load_pair(z_node, 0, "zn")
-        hid[1] = load_part(1, 0, "zh")
-        for s in range(1, PAIRS):
+        for s in range(1, FIRST):
+            hid[s] = load_part(s, 0, "zh")
             zn[s] = load_pair(z_node, s, "zn")
-            if s < 3:
-                cel[s - 1] = load_part(s - 1, CH, "zcc")
-            if s + 1 < PAIRS:
-                load_children(s + 1)
+        for s in range(FIRST, PAIRS):
+            load_children(s)
+            zn[s] = load_pair(z_node, s, "zn")
+            if s < 2 * FIRST:
+                cel[s - FIRST] = load_part(s - FIRST, CH, "zcc")
 
         def t_h(s, i):
             if i == 0:
@@ -119,9 +121,7 @@ def tile_treelstm_pa_kernel(tc, z_node, z_children, W_f, U_f, b_f, out):
             if s < EARLY:
                 sort_words(nc.vector.tensor_copy, sz[:], words)
             else:
-                for tl in range(2):
-                    x = slice(tl * 512, (tl + 1) * 512)
-                    sort_words(nc.scalar.copy, sz[:, x], words[:, x])
+                sort_words(nc.scalar.copy, sz[:], words)
             st["sz", s] = sz
 
         def t_z(s, tl, i):
@@ -214,7 +214,7 @@ def tile_treelstm_pa_kernel(tc, z_node, z_children, W_f, U_f, b_f, out):
 
         def ro_copy(bh):
             accs = work.tile([P, 512], F32, tag="accs", bufs=1, name="accs")
-            nc.scalar.copy(out=accs[:], in_=st["acc", bh][:])
+            (nc.vector.tensor_copy if bh == 0 else nc.scalar.copy)(out=accs[:], in_=st["acc", bh][:])
             st["accs", bh] = accs
 
         def ro_back(bh):
@@ -297,7 +297,6 @@ def tile_treelstm_pa_kernel(tc, z_node, z_children, W_f, U_f, b_f, out):
         for t in range(4):
             x = slice(t * 512, (t + 1) * 512)
             sort_words(nc.vector.tensor_copy, wsort[:, x], wn[:].bitcast(F32)[:, x])
-        sort_z(1)
 
         def mats_of(s, tl):
             return [lambda i=i: mm_plain(s, tl, i) for i in range(5 if s == LAST else 4)]
@@ -305,12 +304,13 @@ def tile_treelstm_pa_kernel(tc, z_node, z_children, W_f, U_f, b_f, out):
         def accs_of(s):
             return [lambda i=i: acc_t(s, i) for i in range(4 if s < LAST - 2 else 8)] if s >= 0 else []
 
-        for mat in mats_of(0, 0):
+        for mat in mats_of(0, 0) + mats_of(0, 1)[:1]:
             mat()
-        weave(mats_of(0, 1), [lambda i=i: t_w(i) for i in range(16)])
+        weave(mats_of(0, 1)[1:], [lambda i=i: t_w(i) for i in range(16)])
         p1(0, 0)
         for q in range(4):
             c_w(q)
+        sort_z(1)
 
         def tiles_of(s):
             lo = 2 * s + sum([1 for x in THIRD if x < s])

@@ -77,14 +77,11 @@ def tile_treelstm_pa_kernel(tc, z_node, z_children, W_f, U_f, b_f, out):
         hid = {}
         cel = {}
         un = const.tile([P, 4 * CH], BF16, name="un")
-        nc.sync.dma_start(
-            out=un[:].rearrange("p (t k) -> p t k", t=4), in_=U_f.rearrange("(t p) k -> p t k", p=P)
-        )
+        nc.sync.dma_start(out=un[:], in_=U_f.rearrange("(p t) k -> p (t k)", t=4))
         hid[0] = load_part(0, 0, "zh")
         wn = const.tile([P, 4 * SIZE], BF16, name="wn")
-        nc.sync.dma_start(
-            out=wn[:].rearrange("p (t k) -> p t k", t=4), in_=W_f.rearrange("(t p) k -> p t k", p=P)
-        )
+        for t in range(4):
+            nc.sync.dma_start(out=wn[:, t * SIZE : (t + 1) * SIZE], in_=W_f[t * P : (t + 1) * P, :])
         zn[0] = load_pair(z_node, 0, "zn")
         for s in range(1, FIRST):
             hid[s] = load_part(s, 0, "zh")
@@ -257,10 +254,11 @@ def tile_treelstm_pa_kernel(tc, z_node, z_children, W_f, U_f, b_f, out):
                     un[:].bitcast(F32)[:, t * 256 + v * P : t * 256 + (v + 1) * P],
                     ident[:],
                 )
-            if v == 0:
-                nc.scalar.copy(out=ut[:, 0:CH], in_=ups[:])
-            else:
-                nc.vector.tensor_copy(out=ut[:, CH:], in_=ups[:])
+            cp = nc.scalar.copy if v == 0 else nc.vector.tensor_copy
+            cp(
+                out=ut[:, v * CH : (v + 1) * CH].rearrange("w (p t) -> w p t", t=4),
+                in_=ups[:].rearrange("w (t p) -> w p t", t=4),
+            )
         ut16 = ut[:].bitcast(BF16).rearrange("p (v c e) -> p v c e", v=2, e=2)
 
         for i in range(4):

@@ -76,9 +76,18 @@ def tile_treelstm_pa_kernel(tc, z_node, z_children, W_f, U_f, b_f, out):
         zn = {}
         hid = {}
         cel = {}
-        un = const.tile([P, 4 * CH], BF16, name="un")
-        nc.sync.dma_start(out=un[:], in_=U_f.rearrange("(p t) k -> p (t k)", t=4))
+        U_rows = U_f.rearrange("(p t) k -> p t k", t=4)
+        un = {}
+
+        def load_u(v):
+            un[v] = const.tile([P, 2 * CH], BF16, name="un%d" % v)
+            nc.sync.dma_start(
+                out=un[v][:].rearrange("p (t k) -> p t k", t=4), in_=U_rows[:, :, v * 256 : (v + 1) * 256]
+            )
+
+        load_u(0)
         hid[0] = load_part(0, 0, "zh")
+        load_u(1)
         wn = const.tile([P, 4 * SIZE], BF16, name="wn")
         for t in range(4):
             nc.sync.dma_start(out=wn[:, t * SIZE : (t + 1) * SIZE], in_=W_f[t * P : (t + 1) * P, :])
@@ -194,7 +203,7 @@ def tile_treelstm_pa_kernel(tc, z_node, z_children, W_f, U_f, b_f, out):
 
         def acc_t(s, i):
             bh, j = divmod(s, PER_HALF)
-            first = j == 0 and i == 0
+            first = ("acc", bh) not in st
             if first:
                 st["acc", bh] = bank("acc", 1)
             nc.tensor.matmul(
@@ -246,29 +255,24 @@ def tile_treelstm_pa_kernel(tc, z_node, z_children, W_f, U_f, b_f, out):
             return steps[:-1] + [last]
 
         ut = const.tile([P, 2 * CH], F32, name="ut")
-        for v in range(2):
-            ups = bank("pl", 2)
+
+        def turn_u(v, eng_copy):
+            bk = bank("mx", 2)
             for t in range(4):
                 nc.tensor.transpose(
-                    ups[:, t * P : (t + 1) * P],
-                    un[:].bitcast(F32)[:, t * 256 + v * P : t * 256 + (v + 1) * P],
-                    ident[:],
+                    bk[:, t * P : (t + 1) * P], un[v][:].bitcast(F32)[:, t * P : (t + 1) * P], ident[:]
                 )
-            cp = nc.scalar.copy if v == 0 else nc.vector.tensor_copy
-            cp(
+            eng_copy(
                 out=ut[:, v * CH : (v + 1) * CH].rearrange("w (p t) -> w p t", t=4),
-                in_=ups[:].rearrange("w (t p) -> w p t", t=4),
+                in_=bk[:].rearrange("w (t p) -> w p t", t=4),
             )
-        ut16 = ut[:].bitcast(BF16).rearrange("p (v c e) -> p v c e", v=2, e=2)
 
+        ut16 = ut[:].bitcast(BF16).rearrange("p (v c e) -> p v c e", v=2, e=2)
+        turn_u(0, nc.vector.tensor_copy)
         for i in range(4):
             t_h(0, i)
         c_h(0)
-
-        bps = bank("acc", 1)
-        nc.tensor.matmul(out=bps[:], lhsT=ones[:], rhs=brow[:], start=True, stop=True)
-        biasb = const.tile([P, CH], F32, name="biasb")
-        nc.vector.tensor_copy(out=biasb[:], in_=bps[:])
+        turn_u(1, nc.vector.tensor_copy)
 
         wg = const.tile([P, 2 * CH * 4], BF16, name="wg", align_bytes=64)
         wq = const.tile([P, 2 * CH], U32, name="wq", align_bytes=64)
@@ -300,11 +304,18 @@ def tile_treelstm_pa_kernel(tc, z_node, z_children, W_f, U_f, b_f, out):
             return [lambda i=i: mm_plain(s, tl, i) for i in range(5 if s == LAST else 4)]
 
         def accs_of(s):
-            return [lambda i=i: acc_t(s, i) for i in range(4 if s < LAST - 2 else 8)] if s >= 0 else []
+            return [lambda i=i: acc_t(s, i) for i in range(4 if s < LAST - 3 else 8)] if s >= 0 else []
 
-        for mat in mats_of(0, 0) + mats_of(0, 1)[:1]:
+        for tl in range(2):
+            for mat in mats_of(0, tl)[:2]:
+                mat()
+        bps = bank("acc", 1)
+        nc.tensor.matmul(out=bps[:], lhsT=ones[:], rhs=brow[:], start=True, stop=True)
+        biasb = const.tile([P, CH], F32, name="biasb")
+        nc.vector.tensor_copy(out=biasb[:], in_=bps[:])
+        for mat in mats_of(0, 0)[2:]:
             mat()
-        weave(mats_of(0, 1)[1:], [lambda i=i: t_w(i) for i in range(16)])
+        weave(mats_of(0, 1)[2:], [lambda i=i: t_w(i) for i in range(16)])
         p1(0, 0)
         for q in range(4):
             c_w(q)
@@ -357,7 +368,7 @@ def tile_treelstm_pa_kernel(tc, z_node, z_children, W_f, U_f, b_f, out):
                 q_z(z)
             for z in sorts_of(s):
                 sort_z(z)
-            if s >= 2:
+            if 2 <= s < LAST - 1:
                 pair_sum(s - 2)
             if m >= 0:
                 p3(m, 0, 1)
@@ -375,14 +386,14 @@ def tile_treelstm_pa_kernel(tc, z_node, z_children, W_f, U_f, b_f, out):
             mat()
         p2(LAST - 1, 0)
         p2(LAST - 1, 1)
-        st["w", LAST] = work.tile([P, 2 * CH], F32, tag="w", bufs=LAG + 2, name="w")
-        nc.scalar.copy(out=st["w", LAST][:, 0:CH], in_=st["pl", LAST, 0][:])
         p3(LAST - 1, 0, 1)
         p3(LAST - 1, 1, 2)
-        nc.scalar.copy(out=half(LAST, 1), in_=st["mx", LAST, 1][:])
+        st["w", LAST] = work.tile([P, 2 * CH], F32, tag="w", bufs=LAG + 2, name="w")
+        nc.scalar.copy(out=st["w", LAST][:, 0:CH], in_=st["pl", LAST, 0][:])
         p4(LAST - 2, 1, 2, nc.vector)
         p2(LAST, 0)
         p3(LAST, 0, 1)
+        nc.scalar.copy(out=half(LAST, 1), in_=st["mx", LAST, 1][:])
         p4(LAST - 1, 0, 1, nc.vector)
         p4(LAST - 1, 1, 2, nc.vector)
         for acc in accs_of(LAST - 3) + accs_of(LAST - 2) + accs_of(LAST - 1):
@@ -393,13 +404,20 @@ def tile_treelstm_pa_kernel(tc, z_node, z_children, W_f, U_f, b_f, out):
             nc.vector.tensor_tensor(out=w[:, x], in0=st["pl", LAST, 1][:, x], in1=w[:, x], op=ADD)
             nc.scalar.activation(out=w[:, x], in_=w[:, x], func=SIGMOID)
         p4(LAST, 0, 1, nc.vector)
-        ro_copy(1)
-        ro_back(1)
+        accs = work.tile([P, 512], F32, tag="accs", bufs=1, name="accs")
+        back = []
+        for k, x in enumerate(parts):
+            nc.scalar.copy(out=accs[:, x], in_=st["acc", 1][:, x])
+            bk = bank(("hps", "mx")[k], k + 1)
+            for cb in range(2):
+                c0 = (2 * k + cb) * P
+                nc.tensor.transpose(bk[:, cb * P : (cb + 1) * P], accs[:, c0 : c0 + P], ident[:])
+            back.append(bk[:, 0 : CH // 2])
         for x in parts:
             nc.vector.tensor_tensor(out=w[:, x], in0=w[:, x], in1=cel[LAST][:, 1, x], op=MULT)
         for x in parts:
             add_v(w[:, x], w[:, x], half(LAST, 0)[:, x])
         res = new_res()
-        for x in parts:
-            add_v(res[:, x], st["ops", 1][:, x], w[:, x])
+        for x, total in zip(parts, back):
+            add_v(res[:, x], total, w[:, x])
             nc.sync.dma_start(out=out[P : 2 * P, x], in_=res[:, x])

@@ -76,18 +76,9 @@ def tile_treelstm_pa_kernel(tc, z_node, z_children, W_f, U_f, b_f, out):
         zn = {}
         hid = {}
         cel = {}
-        U_rows = U_f.rearrange("(p t) k -> p t k", t=4)
-        un = {}
-
-        def load_u(v):
-            un[v] = const.tile([P, 2 * CH], BF16, name="un%d" % v)
-            nc.sync.dma_start(
-                out=un[v][:].rearrange("p (t k) -> p t k", t=4), in_=U_rows[:, :, v * 256 : (v + 1) * 256]
-            )
-
-        load_u(0)
+        un = const.tile([P, 4 * CH], BF16, name="un")
+        nc.sync.dma_start(out=un[:].rearrange("p (t k) -> p t k", t=4), in_=U_f.rearrange("(t p) k -> p t k", t=4))
         hid[0] = load_part(0, 0, "zh")
-        load_u(1)
         wn = const.tile([P, 4 * SIZE], BF16, name="wn")
         for t in range(4):
             nc.sync.dma_start(out=wn[:, t * SIZE : (t + 1) * SIZE], in_=W_f[t * P : (t + 1) * P, :])
@@ -203,7 +194,7 @@ def tile_treelstm_pa_kernel(tc, z_node, z_children, W_f, U_f, b_f, out):
 
         def acc_t(s, i):
             bh, j = divmod(s, PER_HALF)
-            first = ("acc", bh) not in st
+            first = j == 0 and i == 0
             if first:
                 st["acc", bh] = bank("acc", 1)
             nc.tensor.matmul(
@@ -255,24 +246,36 @@ def tile_treelstm_pa_kernel(tc, z_node, z_children, W_f, U_f, b_f, out):
             return steps[:-1] + [last]
 
         ut = const.tile([P, 2 * CH], F32, name="ut")
-
-        def turn_u(v, eng_copy):
-            bk = bank("mx", 2)
-            for t in range(4):
-                nc.tensor.transpose(
-                    bk[:, t * P : (t + 1) * P], un[v][:].bitcast(F32)[:, t * P : (t + 1) * P], ident[:]
-                )
-            eng_copy(
-                out=ut[:, v * CH : (v + 1) * CH].rearrange("w (p t) -> w p t", t=4),
-                in_=bk[:].rearrange("w (t p) -> w p t", t=4),
-            )
-
         ut16 = ut[:].bitcast(BF16).rearrange("p (v c e) -> p v c e", v=2, e=2)
-        turn_u(0, nc.vector.tensor_copy)
-        for i in range(4):
-            t_h(0, i)
-        c_h(0)
-        turn_u(1, nc.vector.tensor_copy)
+        ht0 = work.tile([P, 512], F32, tag="ht", bufs=2, name="ht")
+        st["ht", 0] = ht0[:].bitcast(BF16).rearrange("p (t v r e) -> p t v r e", t=2, v=2, e=2)
+
+        def turn_half(tag, eng_copy, dst, words):
+            bk = bank(tag, 2)
+            for i in range(2):
+                nc.tensor.transpose(bk[:, i * P : (i + 1) * P], words[i], ident[:])
+            eng_copy(out=dst, in_=bk[:, 0:256])
+
+        def turn_u(v):
+            u_words = un[:].bitcast(F32).rearrange("p (t w) -> p t w", t=4)[:, :, v * P : (v + 1) * P]
+            for d in range(2):
+                turn_half(
+                    ("zps", "mx")[d],
+                    (nc.vector.tensor_copy, nc.scalar.copy)[d],
+                    ut[:, v * CH + d * 256 : v * CH + (d + 1) * 256],
+                    [u_words[:, 2 * d + i, :] for i in range(2)],
+                )
+
+        turn_u(0)
+        for tl in range(2):
+            h_words = hid[0][:, tl, :].bitcast(F32)
+            turn_half(
+                "pl",
+                (nc.vector.tensor_copy, nc.scalar.copy)[tl],
+                ht0[:, tl * 256 : (tl + 1) * 256],
+                [h_words[:, v * P : (v + 1) * P] for v in range(2)],
+            )
+        turn_u(1)
 
         wg = const.tile([P, 2 * CH * 4], BF16, name="wg", align_bytes=64)
         wq = const.tile([P, 2 * CH], U32, name="wq", align_bytes=64)
@@ -306,16 +309,14 @@ def tile_treelstm_pa_kernel(tc, z_node, z_children, W_f, U_f, b_f, out):
         def accs_of(s):
             return [lambda i=i: acc_t(s, i) for i in range(4 if s < LAST - 3 else 8)] if s >= 0 else []
 
-        for tl in range(2):
-            for mat in mats_of(0, tl)[:2]:
-                mat()
+        for mat in mats_of(0, 0):
+            mat()
         bps = bank("acc", 1)
         nc.tensor.matmul(out=bps[:], lhsT=ones[:], rhs=brow[:], start=True, stop=True)
         biasb = const.tile([P, CH], F32, name="biasb")
         nc.vector.tensor_copy(out=biasb[:], in_=bps[:])
-        for mat in mats_of(0, 0)[2:]:
-            mat()
-        weave(mats_of(0, 1)[2:], [lambda i=i: t_w(i) for i in range(16)])
+        mats_of(0, 1)[0]()
+        weave(mats_of(0, 1)[1:], [lambda i=i: t_w(i) for i in range(16)])
         p1(0, 0)
         for q in range(4):
             c_w(q)

@@ -307,7 +307,7 @@ def tile_treelstm_pa_kernel(tc, z_node, z_children, W_f, U_f, b_f, out):
             return [lambda i=i: mm_plain(s, tl, i) for i in range(5 if s == LAST else 4)]
 
         def accs_of(s):
-            return [lambda i=i: acc_t(s, i) for i in range(4 if s < LAST - 3 else 8)] if s >= 0 else []
+            return [lambda i=i: acc_t(s, i) for i in range(4 if s < LAST - 2 else 8)] if s >= 0 else []
 
         for mat in mats_of(0, 0):
             mat()
@@ -369,7 +369,7 @@ def tile_treelstm_pa_kernel(tc, z_node, z_children, W_f, U_f, b_f, out):
                 q_z(z)
             for z in sorts_of(s):
                 sort_z(z)
-            if 2 <= s < LAST - 1:
+            if s >= 2:
                 pair_sum(s - 2)
             if m >= 0:
                 p3(m, 0, 1)
@@ -387,14 +387,14 @@ def tile_treelstm_pa_kernel(tc, z_node, z_children, W_f, U_f, b_f, out):
             mat()
         p2(LAST - 1, 0)
         p2(LAST - 1, 1)
-        p3(LAST - 1, 0, 1)
-        p3(LAST - 1, 1, 2)
         st["w", LAST] = work.tile([P, 2 * CH], F32, tag="w", bufs=LAG + 2, name="w")
         nc.scalar.copy(out=st["w", LAST][:, 0:CH], in_=st["pl", LAST, 0][:])
+        p3(LAST - 1, 0, 1)
+        p3(LAST - 1, 1, 2)
+        nc.scalar.copy(out=half(LAST, 1), in_=st["mx", LAST, 1][:])
         p4(LAST - 2, 1, 2, nc.vector)
         p2(LAST, 0)
         p3(LAST, 0, 1)
-        nc.scalar.copy(out=half(LAST, 1), in_=st["mx", LAST, 1][:])
         p4(LAST - 1, 0, 1, nc.vector)
         p4(LAST - 1, 1, 2, nc.vector)
         for acc in accs_of(LAST - 3) + accs_of(LAST - 2) + accs_of(LAST - 1):
@@ -405,20 +405,13 @@ def tile_treelstm_pa_kernel(tc, z_node, z_children, W_f, U_f, b_f, out):
             nc.vector.tensor_tensor(out=w[:, x], in0=st["pl", LAST, 1][:, x], in1=w[:, x], op=ADD)
             nc.scalar.activation(out=w[:, x], in_=w[:, x], func=SIGMOID)
         p4(LAST, 0, 1, nc.vector)
-        accs = work.tile([P, 512], F32, tag="accs", bufs=1, name="accs")
-        back = []
-        for k, x in enumerate(parts):
-            nc.scalar.copy(out=accs[:, x], in_=st["acc", 1][:, x])
-            bk = bank(("hps", "mx")[k], k + 1)
-            for cb in range(2):
-                c0 = (2 * k + cb) * P
-                nc.tensor.transpose(bk[:, cb * P : (cb + 1) * P], accs[:, c0 : c0 + P], ident[:])
-            back.append(bk[:, 0 : CH // 2])
+        ro_copy(1)
+        ro_back(1)
         for x in parts:
             nc.vector.tensor_tensor(out=w[:, x], in0=w[:, x], in1=cel[LAST][:, 1, x], op=MULT)
         for x in parts:
             add_v(w[:, x], w[:, x], half(LAST, 0)[:, x])
         res = new_res()
-        for x, total in zip(parts, back):
-            add_v(res[:, x], total, w[:, x])
+        for x in parts:
+            add_v(res[:, x], st["ops", 1][:, x], w[:, x])
             nc.sync.dma_start(out=out[P : 2 * P, x], in_=res[:, x])

from contextlib import ExitStack

import concourse.mybir as mybir
from concourse.masks import make_identity

F32 = mybir.dt.float32
BF16 = mybir.dt.bfloat16
U32 = mybir.dt.uint32
U8 = mybir.dt.uint8
FP8X4 = mybir.dt.float8_e4m3fn_x4
ADD = mybir.AluOpType.add
MULT = mybir.AluOpType.mult
SIGMOID = mybir.ActivationFunctionType.Sigmoid

P = 128
B, N, SIZE, CH = 256, 16, 1024, 512
FLOPS = 2 * B * N * (SIZE + CH) * CH

PAIRS = 16
PER_HALF = 8
LAST = PAIRS - 1
FIRST = 3
UNSORTED = 1
EARLY = 3
THIRD = (1, 1)
LAG = 4


def tile_treelstm_pa_kernel(tc, z_node, z_children, W_f, U_f, b_f, out):
    nc = tc.nc
    st = {}
    with ExitStack() as ctx:
        const = ctx.enter_context(tc.tile_pool(name="const", bufs=1))
        data = ctx.enter_context(tc.tile_pool(name="data", bufs=1))
        work = ctx.enter_context(tc.tile_pool(name="work", bufs=2))
        psum = ctx.enter_context(tc.psum_pool(name="psum", bufs=1))
        ctx.enter_context(tc.manual_schedule())

        def bank(tag, bufs):
            return psum.tile([P, 512], F32, tag=tag, bufs=bufs, name=tag)

        brow = const.tile([P, CH], BF16, name="brow")
        nc.vector.memset(brow[:], 0.0)
        nc.scalar.dma_start(out=brow[0:1, :], in_=b_f.rearrange("(o c) -> o c", o=1))
        ones = const.tile([P, P], BF16, name="ones")
        nc.vector.memset(ones[:], 1.0)
        warm = const.tile([P, 8], F32, name="warm")
        nc.vector.memset(warm[:], 0.0)
        nc.scalar.activation(out=warm[:], in_=warm[:], func=SIGMOID)
        ident = const.tile([P, P], F32, name="ident")
        make_identity(nc, ident[:])

        def load_pair(src, s, nm):
            bh, j = divmod(s, PER_HALF)
            t = data.tile([P, 2 * SIZE], BF16, name="%s%d" % (nm, s))
            nc.sync.dma_start(
                out=t[:],
                in_=src[bh * P : (bh + 1) * P, 2 * j : 2 * j + 2, :].rearrange("b n k -> b (n k)"),
            )
            return t

        def load_part(s, lo, nm):
            bh, j = divmod(s, PER_HALF)
            t = data.tile([P, 2 * CH], BF16, name="%s%d" % (nm, s))
            nc.sync.dma_start(
                out=t[:].rearrange("p (t k) -> p t k", t=2),
                in_=z_children[bh * P : (bh + 1) * P, 2 * j : 2 * j + 2, lo : lo + CH],
            )
            return t[:].rearrange("p (t k) -> p t k", t=2)

        def load_children(s):
            t = load_pair(z_children, s, "zc")[:].rearrange("p (t k) -> p t k", t=2)
            hid[s] = t[:, :, 0:CH]
            cel[s] = t[:, :, CH:]

        zn = {}
        hid = {}
        cel = {}
        un = const.tile([P, 4 * CH], BF16, name="un")
        nc.sync.dma_start(out=un[:].rearrange("p (t k) -> p t k", t=4), in_=U_f.rearrange("(t p) k -> p t k", t=4))
        hid[0] = load_part(0, 0, "zh")
        wn = const.tile([P, 4 * SIZE], BF16, name="wn")
        for t in range(4):
            nc.sync.dma_start(out=wn[:, t * SIZE : (t + 1) * SIZE], in_=W_f[t * P : (t + 1) * P, :])
        zn[0] = load_pair(z_node, 0, "zn")
        for s in range(1, FIRST):
            hid[s] = load_part(s, 0, "zh")
            zn[s] = load_pair(z_node, s, "zn")
        for s in range(FIRST, PAIRS):
            load_children(s)
            zn[s] = load_pair(z_node, s, "zn")
            if s < 2 * FIRST:
                cel[s - FIRST] = load_part(s - FIRST, CH, "zcc")

        def t_h(s, i):
            if i == 0:
                st["hps", s] = bank("hps", 1)
            tl, v = divmod(i, 2)
            nc.tensor.transpose(
                st["hps", s][:, i * P : (i + 1) * P],
                hid[s][:, tl, :].bitcast(F32)[:, v * P : (v + 1) * P],
                ident[:],
            )

        def c_h(s):
            ht = work.tile([P, 512], F32, tag="ht", bufs=2, name="ht")
            nc.scalar.copy(out=ht[:], in_=st["hps", s][:])
            st["ht", s] = ht[:].bitcast(BF16).rearrange("p (t v r e) -> p t v r e", t=2, v=2, e=2)

        def sort_words(eng_copy, dst, src):
            eng_copy(
                out=dst.rearrange("p (q u r) -> p q u r", u=2, r=P), in_=src.rearrange("p (q r u) -> p q u r", u=2, r=P)
            )

        def sort_z(s):
            sz = work.tile([P, SIZE], F32, tag="sz", bufs=3, name="sz")
            words = zn[s][:].bitcast(F32)
            if s < EARLY:
                sort_words(nc.vector.tensor_copy, sz[:], words)
            else:
                sort_words(nc.scalar.copy, sz[:], words)
            st["sz", s] = sz

        def t_z(s, tl, i):
            g, u = divmod(i, 2)
            if i == 0:
                st["zps", s, tl] = bank("zps", 2)
            if s < UNSORTED:
                words = zn[s][:].bitcast(F32)[:, tl * 512 + g * 256 + u : tl * 512 + (g + 1) * 256 : 2]
            else:
                words = st["sz", s][:, tl * 512 + i * P : tl * 512 + (i + 1) * P]
            nc.tensor.transpose(st["zps", s, tl][:, i * P : (i + 1) * P], words, ident[:])

        def c_z(s, tl):
            if tl == 0:
                st["zg", s] = work.tile([P, 2048], BF16, tag="zg", bufs=2, name="zg", align_bytes=64)
            dst = st["zg", s][:].bitcast(F32)[:, tl * 512 : (tl + 1) * 512]
            nc.scalar.copy(
                out=dst.rearrange("p (g r u) -> p g r u", g=2, u=2),
                in_=st["zps", s, tl][:].rearrange("p (g u r) -> p g r u", g=2, u=2),
            )

        def q_z(s):
            zq = work.tile([P, 512], U32, tag="zq", bufs=4, name="zq", align_bytes=64)
            zs = work.tile([P, 512], U8, tag="zs", bufs=4, name="zs", align_bytes=64)
            nc.vector.quantize_mx(out=zq[:].bitcast(FP8X4), scales=zs[:], in_=st["zg", s][:])
            st["zq", s] = (zq, zs)

        def mm_plain(s, tl, i):
            if i == 0:
                st["pl", s, tl] = bank("pl", 2)
            v, e = divmod(i, 2)
            ops = (st["ht", s][:, tl, v, :, e], ut16[:, v, :, e]) if i < 4 else (ones[:], brow[:])
            nc.tensor.matmul(
                out=st["pl", s, tl][:], lhsT=ops[0], rhs=ops[1], start=(i == 0), stop=(i == (4 if s == LAST else 3))
            )

        def mm_mx(s, tl, tag="mx"):
            st["mx", s, tl] = bank(tag, 2)
            zq, zs = st["zq", s]
            for g in range(2):
                c0 = (tl * 2 + g) * P
                nc.tensor.matmul_mx(
                    out=st["mx", s, tl][:],
                    lhsT=zq[:, c0 : c0 + P].bitcast(FP8X4),
                    lhsT_scale=zs[:, c0 : c0 + P],
                    rhs=wq[:, g * CH : (g + 1) * CH].bitcast(FP8X4),
                    rhs_scale=ws[:, g * CH : (g + 1) * CH],
                    start=(g == 0),
                    stop=(g == 1),
                )

        def half(s, tl):
            return st["w", s][:, tl * CH : (tl + 1) * CH]

        def p1(s, tl):
            if tl == 0:
                st["w", s] = work.tile([P, 2 * CH], F32, tag="w", bufs=LAG + 2, name="w")
            nc.vector.tensor_tensor(out=half(s, tl), in0=st["pl", s, tl][:], in1=biasb[:], op=ADD)

        def p2(s, tl):
            nc.vector.tensor_tensor(out=half(s, tl), in0=st["mx", s, tl][:], in1=half(s, tl), op=ADD)

        def p3(s, lo, hi):
            w = st["w", s][:, lo * CH : hi * CH]
            nc.scalar.activation(out=w, in_=w, func=SIGMOID)

        def p4(s, lo, hi, eng):
            w3 = st["w", s][:].rearrange("p (t c) -> p t c", t=2)[:, lo:hi, :]
            eng.tensor_tensor(out=w3, in0=w3, in1=cel[s][:, lo:hi, :], op=MULT)

        def pair_sum(s):
            nc.vector.tensor_tensor(out=half(s, 0), in0=half(s, 0), in1=half(s, 1), op=ADD)

        def acc_t(s, i):
            bh, j = divmod(s, PER_HALF)
            first = j == 0 and i == 0
            if first:
                st["acc", bh] = bank("acc", 1)
            nc.tensor.matmul(
                out=st["acc", bh][:, i % 4 * P : (i % 4 + 1) * P],
                lhsT=st["w", s][:, i * P : (i + 1) * P],
                rhs=ident[:],
                is_transpose=True,
                start=first,
                stop=((s, i) in ((PER_HALF - 1, 3), (LAST - 1, 7))),
            )

        def store(bh, res):
            nc.sync.dma_start(out=out[bh * P : (bh + 1) * P, :], in_=res[:])

        def ro_copy(bh):
            accs = work.tile([P, 512], F32, tag="accs", bufs=1, name="accs")
            (nc.vector.tensor_copy if bh == 0 else nc.scalar.copy)(out=accs[:], in_=st["acc", bh][:])
            st["accs", bh] = accs

        def ro_back(bh):
            ops = bank("hps", 1)
            st["ops", bh] = ops
            for cb in range(4):
                nc.tensor.transpose(
                    ops[:, cb * P : (cb + 1) * P], st["accs", bh][:, cb * P : (cb + 1) * P], ident[:]
                )

        def new_res():
            return work.tile([P, CH], F32, tag="res", bufs=2, name="res")

        def add_v(dst, x, y):
            nc.vector.tensor_tensor(out=dst, in0=x, in1=y, op=ADD)

        def weave(mats, trans):
            gaps = len(mats) - 1
            done = 0
            for i, m in enumerate(mats):
                m()
                upto = min(len(trans), (len(trans) * (i + 1) + gaps - 1) // gaps)
                while done < upto:
                    trans[done]()
                    done += 1

        def turn(steps, copy):
            def last():
                steps[-1]()
                copy()

            return steps[:-1] + [last]

        ut = const.tile([P, 2 * CH], F32, name="ut")
        ut16 = ut[:].bitcast(BF16).rearrange("p (v c e) -> p v c e", v=2, e=2)
        ht0 = work.tile([P, 512], F32, tag="ht", bufs=2, name="ht")
        st["ht", 0] = ht0[:].bitcast(BF16).rearrange("p (t v r e) -> p t v r e", t=2, v=2, e=2)

        def turn_half(tag, eng_copy, dst, words):
            bk = bank(tag, 2)
            for i in range(2):
                nc.tensor.transpose(bk[:, i * P : (i + 1) * P], words[i], ident[:])
            eng_copy(out=dst, in_=bk[:, 0:256])

        def turn_u(v):
            u_words = un[:].bitcast(F32).rearrange("p (t w) -> p t w", t=4)[:, :, v * P : (v + 1) * P]
            for d in range(2):
                turn_half(
                    ("zps", "mx")[d],
                    (nc.vector.tensor_copy, nc.scalar.copy)[d],
                    ut[:, v * CH + d * 256 : v * CH + (d + 1) * 256],
                    [u_words[:, 2 * d + i, :] for i in range(2)],
                )

        turn_u(0)
        for tl in range(2):
            h_words = hid[0][:, tl, :].bitcast(F32)
            turn_half(
                "pl",
                (nc.vector.tensor_copy, nc.scalar.copy)[tl],
                ht0[:, tl * 256 : (tl + 1) * 256],
                [h_words[:, v * P : (v + 1) * P] for v in range(2)],
            )
        turn_u(1)

        wg = const.tile([P, 2 * CH * 4], BF16, name="wg", align_bytes=64)
        wq = const.tile([P, 2 * CH], U32, name="wq", align_bytes=64)
        ws = const.tile([P, 2 * CH], U8, name="ws", align_bytes=64)

        def t_w(i):
            q, r = divmod(i, 4)
            g, hh = divmod(q, 2)
            u, t = divmod(r, 2)
            if r == 0:
                st["wps", q] = bank(("zps", "mx")[q % 2], 2)
            c0 = (2 * hh + t) * 512 + (2 * g + u) * P
            nc.tensor.transpose(st["wps", q][:, r * P : (r + 1) * P], wsort[:, c0 : c0 + P], ident[:])

        def c_w(q):
            src = st["wps", q][:].rearrange("p (u x) -> p x u", u=2)
            dst = wg[:].bitcast(F32)[:, q * 512 : (q + 1) * 512].rearrange("p (x u) -> p x u", u=2)
            if q % 2 == 0:
                nc.scalar.copy(out=dst, in_=src)
            else:
                nc.vector.tensor_copy(out=dst, in_=src)

        wsort = const.tile([P, 4 * 512], F32, name="wsort")
        for t in range(4):
            x = slice(t * 512, (t + 1) * 512)
            sort_words(nc.vector.tensor_copy, wsort[:, x], wn[:].bitcast(F32)[:, x])

        def mats_of(s, tl):
            return [lambda i=i: mm_plain(s, tl, i) for i in range(5 if s == LAST else 4)]

        def accs_of(s):
            return [lambda i=i: acc_t(s, i) for i in range(4 if s < LAST - 2 else 8)] if s >= 0 else []

        for mat in mats_of(0, 0):
            mat()
        bps = bank("acc", 1)
        nc.tensor.matmul(out=bps[:], lhsT=ones[:], rhs=brow[:], start=True, stop=True)
        biasb = const.tile([P, CH], F32, name="biasb")
        nc.vector.tensor_copy(out=biasb[:], in_=bps[:])
        mats_of(0, 1)[0]()
        weave(mats_of(0, 1)[1:], [lambda i=i: t_w(i) for i in range(16)])
        p1(0, 0)
        for q in range(4):
            c_w(q)
        sort_z(1)

        def tiles_of(s):
            lo = 2 * s + sum([1 for x in THIRD if x < s])
            hi = 2 * s + 2 + sum([1 for x in THIRD if x <= s])
            return range(lo, min(hi, 2 * PAIRS)) if s < LAST else []

        def whole(s):
            return [t // 2 for t in tiles_of(s) if t % 2 == 1]

        def sorts_of(s):
            return [t // 2 for t in tiles_of(s + 1) if t % 2 == 0 and t // 2 >= EARLY]

        for s in range(LAST):
            a = s - LAG
            m = s - 1
            steps = turn([lambda i=i: t_h(s + 1, i) for i in range(4)], lambda: c_h(s + 1)) + accs_of(a)
            for t in tiles_of(s):
                z, tl = divmod(t, 2)
                steps += turn(
                    [lambda z=z, tl=tl, i=i: t_z(z, tl, i) for i in range(4)], lambda z=z, tl=tl: c_z(z, tl)
                )
            if s == 0:
                for step in steps:
                    step()
            else:
                weave(mats_of(s, 0) + mats_of(s, 1), steps)
            if a == PER_HALF:
                ro_back(0)
                res = new_res()
                nc.scalar.copy(out=res[:], in_=st["ops", 0][:])
                store(0, res)
            if a == PER_HALF - 1:
                ro_copy(0)
            if s > 0:
                p1(s, 0)
            p1(s, 1)
            if m >= 0:
                for tl in range(2):
                    mm_mx(m, tl)
                p2(m, 0)
                p2(m, 1)
            if s == 0:
                sort_z(2)
                nc.vector.quantize_mx(out=wq[:].bitcast(FP8X4), scales=ws[:], in_=wg[:])
            for z in whole(s):
                q_z(z)
            for z in sorts_of(s):
                sort_z(z)
            if s >= 2:
                pair_sum(s - 2)
            if m >= 0:
                p3(m, 0, 1)
                p4(m, 0, 1, nc.gpsimd)
                p3(m, 1, 2)
                if s < LAST - 1:
                    p4(m, 1, 2, nc.gpsimd)

        mm_mx(LAST - 1, 0, "zps")
        mm_mx(LAST - 1, 1, "zps")
        weave(mats_of(LAST, 0), accs_of(LAST - LAG))
        mm_mx(LAST, 0)
        mm_mx(LAST, 1)
        for mat in mats_of(LAST, 1):
            mat()
        p2(LAST - 1, 0)
        p2(LAST - 1, 1)
        st["w", LAST] = work.tile([P, 2 * CH], F32, tag="w", bufs=LAG + 2, name="w")
        nc.scalar.copy(out=st["w", LAST][:, 0:CH], in_=st["pl", LAST, 0][:])
        p3(LAST - 1, 0, 1)
        p3(LAST - 1, 1, 2)
        nc.scalar.copy(out=half(LAST, 1), in_=st["mx", LAST, 1][:])
        p4(LAST - 2, 1, 2, nc.vector)
        p2(LAST, 0)
        p3(LAST, 0, 1)
        p4(LAST - 1, 0, 1, nc.vector)
        p4(LAST - 1, 1, 2, nc.vector)
        for acc in accs_of(LAST - 3) + accs_of(LAST - 2) + accs_of(LAST - 1):
            acc()
        w = half(LAST, 1)
        parts = [slice(0, CH // 2), slice(CH // 2, CH)]
        for x in parts:
            nc.vector.tensor_tensor(out=w[:, x], in0=st["pl", LAST, 1][:, x], in1=w[:, x], op=ADD)
            nc.scalar.activation(out=w[:, x], in_=w[:, x], func=SIGMOID)
        p4(LAST, 0, 1, nc.vector)
        ro_copy(1)
        ro_back(1)
        for x in parts:
            nc.vector.tensor_tensor(out=w[:, x], in0=w[:, x], in1=cel[LAST][:, 1, x], op=MULT)
        for x in parts:
            add_v(w[:, x], w[:, x], half(LAST, 0)[:, x])
        res = new_res()
        for x in parts:
            add_v(res[:, x], st["ops", 1][:, x], w[:, x])
            nc.sync.dma_start(out=out[P : 2 * P, x], in_=res[:, x])
